import numpy as np
import ml_dtypes


def mxq(x, axis, fmt="e4m3"):
    dtype, down = {"e4m3": (ml_dtypes.float8_e4m3fn, 7), "e5m2": (ml_dtypes.float8_e5m2, 14)}[fmt]
    v = np.moveaxis(np.asarray(x, np.float32).astype(ml_dtypes.bfloat16).astype(np.float64), axis, -1)
    blocks = v.reshape(v.shape[:-1] + (-1, 32))
    amax = np.abs(blocks).max(-1, keepdims=True)
    byte = np.maximum(np.where(amax > 0, np.frexp(amax)[1] - 1 + 127, 0) - down, 1)
    scale = np.exp2(byte - 127.0)
    codes = (blocks / scale).astype(np.float32).astype(dtype).astype(np.float64)
    return np.moveaxis((codes * scale).reshape(v.shape), -1, axis)


WIDE = False


def mx_kscale(k):
    if not WIDE:
        return np.ones(k)
    levels = np.array([10, -10, 5, -5, 0])
    a = np.random.permutation(np.resize(levels, k // 512 * 4)).reshape(k // 512, 4)
    idx = np.arange(k)
    return np.exp2(a[idx // 512, idx % 128 // 32])


BF16 = ml_dtypes.bfloat16


def bf(x):
    return np.asarray(x, np.float32).astype(BF16)


def f64(x):
    return np.asarray(x).astype(np.float64)


E2M1 = np.array([0.0, 0.5, 1.0, 1.5, 2.0, 3.0, 4.0, 6.0, -0.0, -0.5, -1.0, -1.5, -2.0, -3.0, -4.0, -6.0])


def pack_weight(w, fmt):
    k, n = w.shape
    w = f64(bf(w)).reshape(k // 32, 32, n)
    amax = np.abs(w).max(1)
    if fmt == "e4m3":
        byte = np.frexp(amax)[1] - 1 + 127 - 7
    else:
        mant, ex = np.frexp(amax / 6.0)
        byte = np.where(mant > 0.5, ex, ex - 1) + 127
    byte = np.clip(np.where(amax > 0, byte, 1), 1, 254)
    scaled = (w * np.exp2(127.0 - byte)[:, None, :]).reshape(k, n).astype(np.float32)
    by_word = np.ascontiguousarray(scaled.reshape(k // 512, 128, 4, n).transpose(0, 1, 3, 2))
    if fmt == "e4m3":
        words = by_word.astype(ml_dtypes.float8_e4m3fn).view(np.uint8)
    else:
        c = by_word.astype(ml_dtypes.float4_e2m1fn).view(np.uint8) & 0xF
        words = c[..., 0::2] | (c[..., 1::2] << 4)
    return np.ascontiguousarray(words), np.ascontiguousarray(byte.astype(np.uint8).reshape(k // 512, 16, n))


def unpack_weight(words, scales, fmt):
    g, p, n, _ = words.shape
    if fmt == "e4m3":
        vals = np.ascontiguousarray(words).view(ml_dtypes.float8_e4m3fn).astype(np.float64)
    else:
        nib = np.empty((g, p, n, 4), np.uint8)
        nib[..., 0::2] = words & 0xF
        nib[..., 1::2] = words >> 4
        vals = E2M1[nib]
    vals = vals * np.repeat(np.exp2(scales.astype(np.float64) - 127.0), 8, axis=1)[..., None]
    return vals.transpose(0, 1, 3, 2).reshape(g * 512, n)


B, I, H, AH, AI, G = 256, 8192, 8192, 128, 128, 4
EPS = 1e-5
K = I + H


def sigmoid(v):
    return 1.0 / (1.0 + np.exp(-v))


def ln(v, w, b):
    mu = v.mean(-1, keepdims=True)
    var = ((v - mu) ** 2).mean(-1, keepdims=True)
    return (v - mu) / np.sqrt(var + EPS) * w + b


def setup_inputs():
    n = np.random.standard_normal
    s = mx_kscale(K)
    x = bf(n((B, I)) * s[:I])
    hx = bf(n((B, H)) * s[I:])
    ah = bf(n((B, AH)))
    ac = bf(n((B, AH)))
    a_w_ih_words, a_w_ih_scales = pack_weight((n((G * AH, K)) / np.sqrt(K) / s).T, "e4m3")
    return {
        "x": x,
        "hx": hx,
        "ah": ah,
        "ac": ac,
        "a_w_ih_words": a_w_ih_words,
        "a_w_ih_scales": a_w_ih_scales,
        "a_w_hh": bf(n((G * AH, AH)) / np.sqrt(AH)),
        "a_ln_i_w": bf(1.0 + 0.1 * n(G * AH)),
        "a_ln_i_b": bf(0.2 * n(G * AH)),
        "a_ln_h_w": bf(1.0 + 0.1 * n(G * AH)),
        "a_ln_h_b": bf(0.2 * n(G * AH)),
        "a_ln_c_w": bf(1.0 + 0.1 * n(AH)),
        "a_ln_c_b": bf(0.2 * n(AH)),
    }


def reference(x, hx, ah, ac, a_w_ih_words, a_w_ih_scales, a_w_hh, a_ln_i_w, a_ln_i_b, a_ln_h_w, a_ln_h_b, a_ln_c_w, a_ln_c_b):
    ai = np.concatenate([f64(x), f64(hx)], axis=1)
    ig = ln(mxq(ai, 1, "e4m3") @ unpack_weight(a_w_ih_words, a_w_ih_scales, "e4m3"), f64(a_ln_i_w), f64(a_ln_i_b))
    hg = ln(f64(ah) @ f64(a_w_hh).T, f64(a_ln_h_w), f64(a_ln_h_b))
    g = ig + hg
    gi, gf, gj, go = np.split(g, G, axis=1)
    acy = ln(sigmoid(gf) * f64(ac) + sigmoid(gi) * np.tanh(gj), f64(a_ln_c_w), f64(a_ln_c_b))
    ada = sigmoid(go) * np.tanh(acy)
    return ada, acy

@@ -1,0 +1,329 @@
+from contextlib import ExitStack
+
+import concourse.masks as masks
+import concourse.mybir as mybir
+
+BF16 = mybir.dt.bfloat16
+F32 = mybir.dt.float32
+I32 = mybir.dt.int32
+U32 = mybir.dt.uint32
+U8 = mybir.dt.uint8
+FP8X4 = mybir.dt.float8_e4m3fn_x4
+ALU = mybir.AluOpType
+ACT = mybir.ActivationFunctionType
+
+P = 128
+BATCH = 256
+BATCH_TILES = BATCH // P
+FEATURES = 8192
+K = 2 * FEATURES
+PACK = 4
+K_PASS = P * PACK
+PASSES = K // K_PASS
+GATE_COLS = 512
+CELL = 128
+EPS = 1e-5
+
+FLOPS = 2 * BATCH * K * GATE_COLS + 2 * BATCH * CELL * GATE_COLS
+
+CHUNK_PASSES = 4
+CHUNK_COLS = CHUNK_PASSES * K_PASS
+CHUNKS = PASSES // CHUNK_PASSES
+CHUNKS_IN_X = FEATURES // CHUNK_COLS
+BANK_PASSES = 2
+WORDS_PASS = K_PASS // 2
+
+COPY_ROUND = 4
+
+W_LOAD_PASSES = 2
+
+PLANE_PASSES = 4
+PLANE_STEP = 4
+QUADRANTS = 4
+QUADRANT = P // QUADRANTS
+
+GAIN_I = 0
+GAIN_H = GAIN_I + GATE_COLS
+SHIFT_G = GAIN_H + GATE_COLS
+GAIN_C = SHIFT_G + GATE_COLS
+SHIFT_C = GAIN_C + CELL
+ROW_COLS = SHIFT_C + CELL
+
+
+def as_row(vector):
+    return vector.rearrange("(o n) -> o n", o=1)
+
+
+def transpose_chunk(nc, banks, ai_tile, ident_words):
+    words = ai_tile[:].bitcast(F32)
+    filled = []
+    for half in range(CHUNK_PASSES // BANK_PASSES):
+        bank = banks.tile([P, BANK_PASSES, 2, P], F32, tag="bank")
+        for i in range(BANK_PASSES):
+            first = (half * BANK_PASSES + i) * WORDS_PASS
+            for u in range(2):
+                nc.tensor.transpose(
+                    out=bank[:, i, u, :],
+                    in_=words[:, first + u : first + WORDS_PASS : 2],
+                    identity=ident_words[:],
+                )
+        filled.append(bank)
+    return filled
+
+
+def regroup_chunk(nc, grouped, filled, first_bank):
+    grouped_words = grouped[:].bitcast(F32)
+    for half, bank in enumerate(filled):
+        out = grouped_words[:, half * BANK_PASSES : (half + 1) * BANK_PASSES, :, :]
+        in_ = bank[:].rearrange("p i u b -> p i b u")
+        if (first_bank + half) % COPY_ROUND == COPY_ROUND - 1:
+            nc.vector.tensor_copy(out=out, in_=in_)
+        else:
+            nc.scalar.copy(out=out, in_=in_)
+
+
+def moments(nc, small, neg_half, values):
+    stats = small.tile([P, 6], F32)
+    nc.vector.bn_stats(out=stats[:], in_=values)
+    mean_var = small.tile([P, 2], F32)
+    nc.vector.bn_aggr(out=mean_var[:], in_=stats[:])
+    var_eps = small.tile([P, 1], F32)
+    nc.vector.tensor_scalar_add(out=var_eps[:], in0=mean_var[:, 1:2], scalar1=EPS)
+    rstd = small.tile([P, 1], F32)
+    nc.gpsimd.tensor_tensor(out=rstd[:], in0=var_eps[:], in1=neg_half[:], op=ALU.pow)
+    return mean_var[:, 0:1], rstd[:]
+
+
+def normalise(nc, out, centred, values, mean, rstd, gain, shift):
+    nc.vector.scalar_tensor_tensor(out=centred, in0=values, scalar=mean, in1=gain, op0=ALU.subtract, op1=ALU.mult)
+    nc.vector.scalar_tensor_tensor(out=out, in0=centred, scalar=rstd, in1=shift, op0=ALU.mult, op1=ALU.add)
+
+
+def tile_adaptivelstmcell_pa_k_kernel(
+    tc,
+    x,
+    hx,
+    ah,
+    ac,
+    a_w_ih_words,
+    a_w_ih_scales,
+    a_w_hh,
+    a_ln_i_w,
+    a_ln_i_b,
+    a_ln_h_w,
+    a_ln_h_b,
+    a_ln_c_w,
+    a_ln_c_b,
+    out_0,
+    out_1,
+):
+    nc = tc.nc
+    tiles = range(BATCH_TILES)
+    with ExitStack() as ctx:
+        ctx.enter_context(tc.manual_schedule())
+        keep = ctx.enter_context(tc.tile_pool(name="keep", bufs=1))
+        stage = ctx.enter_context(tc.tile_pool(name="stage", bufs=3))
+        small = ctx.enter_context(tc.tile_pool(name="small", bufs=4))
+        banks = ctx.enter_context(tc.psum_pool(name="banks", bufs=6))
+        sums = ctx.enter_context(tc.psum_pool(name="sums", bufs=1))
+
+        w_planes = keep.tile([P, PASSES // PLANE_PASSES, GATE_COLS], U8, align_bytes=64)
+        nc.vector.memset(w_planes[:].bitcast(I32), 0)
+        rows = keep.tile([P, ROW_COLS], BF16)
+        nc.vector.memset(rows[:], 0.0)
+        ones = keep.tile([P, P], BF16)
+        nc.vector.memset(ones[:], 1.0)
+        neg_half = keep.tile([P, 1], F32)
+        nc.vector.memset(neg_half[:], -0.5)
+        ident_words = keep.tile([P, P], F32)
+        masks.make_identity(nc, ident_words[:])
+        ident_bf16 = keep.tile([P, P], BF16)
+        masks.make_identity(nc, ident_bf16[:])
+        table_warmer = keep.tile([P, 1], F32)
+        nc.scalar.activation(out=table_warmer[:], in_=neg_half[:], func=ACT.Sigmoid)
+
+        ai_tiles = {}
+        for chunk in range(CHUNKS):
+            source = x if chunk < CHUNKS_IN_X else hx
+            first = (chunk % CHUNKS_IN_X) * CHUNK_COLS
+            for bt in tiles:
+                ai_tile = keep.tile([P, CHUNK_COLS], BF16, name="ai_%d_%d" % (chunk, bt))
+                nc.sync.dma_start(out=ai_tile[:], in_=source[bt * P : (bt + 1) * P, first : first + CHUNK_COLS])
+                ai_tiles[(chunk, bt)] = ai_tile
+
+        for quadrant in range(QUADRANTS):
+            for r in range(PLANE_STEP):
+                start = quadrant * QUADRANT + r
+                nc.sync.dma_start(
+                    out=w_planes[start : start + PLANE_PASSES * PLANE_STEP : PLANE_STEP, :, :].bitcast(I32),
+                    in_=a_w_ih_scales[:, quadrant * PLANE_STEP + r, :]
+                    .rearrange("(j i) n -> i j n", i=PLANE_PASSES)
+                    .bitcast(I32),
+                )
+
+        w_tiles = []
+        for first_pass in range(0, PASSES, W_LOAD_PASSES):
+            w_tile = keep.tile([P, W_LOAD_PASSES, GATE_COLS], U32, name="w_%d" % first_pass, align_bytes=64)
+            nc.sync.dma_start(
+                out=w_tile[:].bitcast(I32),
+                in_=a_w_ih_words[first_pass : first_pass + W_LOAD_PASSES]
+                .rearrange("g p n t -> p g (n t)")
+                .bitcast(I32),
+            )
+            w_tiles.append(w_tile)
+
+        ah_sb = keep.tile([P, BATCH_TILES, CELL], BF16)
+        nc.gpsimd.dma_start(out=ah_sb[:], in_=ah.rearrange("(t p) k -> p t k", p=P))
+        whh_sb = keep.tile([P, GATE_COLS // P, CELL], BF16)
+        nc.gpsimd.dma_start(out=whh_sb[:], in_=a_w_hh.rearrange("(c p) k -> p c k", p=P))
+        nc.gpsimd.dma_start(out=rows[0:1, GAIN_H : GAIN_H + GATE_COLS], in_=as_row(a_ln_h_w))
+        nc.gpsimd.dma_start(out=rows[0:1, SHIFT_G : SHIFT_G + GATE_COLS], in_=as_row(a_ln_i_b))
+        nc.gpsimd.dma_start(out=rows[1:2, SHIFT_G : SHIFT_G + GATE_COLS], in_=as_row(a_ln_h_b))
+        nc.gpsimd.dma_start(out=rows[0:1, GAIN_I : GAIN_I + GATE_COLS], in_=as_row(a_ln_i_w))
+        nc.gpsimd.dma_start(out=rows[0:1, GAIN_C : GAIN_C + CELL], in_=as_row(a_ln_c_w))
+        nc.gpsimd.dma_start(out=rows[0:1, SHIFT_C : SHIFT_C + CELL], in_=as_row(a_ln_c_b))
+        ac_sb = keep.tile([P, BATCH_TILES, CELL], BF16)
+        nc.gpsimd.dma_start(out=ac_sb[:], in_=ac.rearrange("(t p) c -> p t c", p=P))
+
+        ai_codes = {}
+        ai_scales = {}
+
+        def quantise_chunk(key, grouped):
+            codes = keep.tile([P, CHUNK_PASSES * P], U32, name="codes_%d_%d" % key, align_bytes=64)
+            scales = keep.tile([P, CHUNK_PASSES * P], U8, name="scales_%d_%d" % key, align_bytes=64)
+            nc.vector.quantize_mx(
+                out=codes[:].bitcast(FP8X4),
+                scales=scales[:],
+                in_=grouped[:].rearrange("p i b t -> p (i b t)"),
+            )
+            ai_codes[key] = codes
+            ai_scales[key] = scales
+
+        regrouped = None
+        for step, key in enumerate([(chunk, bt) for chunk in range(CHUNKS) for bt in tiles]):
+            filled = transpose_chunk(nc, banks, ai_tiles[key], ident_words)
+            if regrouped is not None:
+                quantise_chunk(regrouped[0], regrouped[1])
+            grouped = stage.tile([P, CHUNK_PASSES, P, PACK], BF16, align_bytes=64)
+            regroup_chunk(nc, grouped, filled, step * len(filled))
+            regrouped = (key, grouped)
+        quantise_chunk(regrouped[0], regrouped[1])
+
+        k_first_ps = banks.tile([P, BATCH_TILES + GATE_COLS // P, P], BF16, tag="bank")
+        for bt in tiles:
+            nc.tensor.transpose(out=k_first_ps[:, bt, :], in_=ah_sb[:, bt, :], identity=ident_bf16[:])
+        for c in range(GATE_COLS // P):
+            nc.tensor.transpose(out=k_first_ps[:, BATCH_TILES + c, :], in_=whh_sb[:, c, :], identity=ident_bf16[:])
+        k_first = keep.tile([P, BATCH_TILES + GATE_COLS // P, P], BF16)
+        nc.scalar.copy(out=k_first[:], in_=k_first_ps[:])
+
+        spread = keep.tile([P, ROW_COLS], F32)
+        for first in range(0, ROW_COLS, GATE_COLS):
+            width = min(GATE_COLS, ROW_COLS - first)
+            spread_ps = banks.tile([P, GATE_COLS], F32, tag="bank")
+            nc.tensor.matmul(
+                out=spread_ps[:, :width], lhsT=ones[:], rhs=rows[:, first : first + width], start=True, stop=True
+            )
+            nc.scalar.copy(out=spread[:, first : first + width], in_=spread_ps[:, :width])
+
+        hg_ps = []
+        hg_moments = []
+        for bt in tiles:
+            hg = banks.tile([P, GATE_COLS], F32, tag="bank")
+            nc.tensor.matmul(
+                out=hg[:],
+                lhsT=k_first[:, bt, :],
+                rhs=k_first[:, BATCH_TILES:, :].rearrange("p c n -> p (c n)"),
+                start=True,
+                stop=True,
+            )
+            hg_ps.append(hg)
+            hg_moments.append(moments(nc, small, neg_half, hg[:]))
+        hg_shift = []
+        for bt in tiles:
+            mean, rstd = hg_moments[bt]
+            centred = stage.tile([P, GATE_COLS], F32, tag="centred")
+            shifted = keep.tile([P, GATE_COLS], F32, name="hg_shift_%d" % bt)
+            normalise(
+                nc,
+                shifted[:],
+                centred[:],
+                hg_ps[bt][:],
+                mean,
+                rstd,
+                spread[:, GAIN_H : GAIN_H + GATE_COLS],
+                spread[:, SHIFT_G : SHIFT_G + GATE_COLS],
+            )
+            hg_shift.append(shifted)
+
+        ig_ps = [sums.tile([P, GATE_COLS], F32, name="ig_%d" % bt) for bt in tiles]
+        for g in range(PASSES):
+            w_tile = w_tiles[g // W_LOAD_PASSES]
+            plane_start = (g % PLANE_PASSES) * PLANE_STEP
+            in_chunk = slice((g % CHUNK_PASSES) * P, (g % CHUNK_PASSES + 1) * P)
+            for bt in tiles:
+                key = (g // CHUNK_PASSES, bt)
+                nc.tensor.matmul_mx(
+                    out=ig_ps[bt][:],
+                    lhsT=ai_codes[key][:, in_chunk].bitcast(FP8X4),
+                    lhsT_scale=ai_scales[key][:, in_chunk],
+                    rhs=w_tile[:, g % W_LOAD_PASSES, :].bitcast(FP8X4),
+                    rhs_scale=w_planes[plane_start:P, g // PLANE_PASSES, :],
+                    start=(g == 0),
+                    stop=(g == PASSES - 1),
+                )
+
+        ig_moments = [moments(nc, small, neg_half, ig_ps[bt][:]) for bt in tiles]
+        gates = []
+        for bt in tiles:
+            mean, rstd = ig_moments[bt]
+            centred = stage.tile([P, GATE_COLS], F32, tag="centred")
+            g_sum = keep.tile([P, GATE_COLS], F32, name="g_sum_%d" % bt)
+            normalise(
+                nc, g_sum[:], centred[:], ig_ps[bt][:], mean, rstd, spread[:, GAIN_I : GAIN_I + GATE_COLS], hg_shift[bt][:]
+            )
+            gates.append(g_sum)
+
+        for bt in tiles:
+            nc.scalar.activation(out=gates[bt][:, : 2 * CELL], in_=gates[bt][:, : 2 * CELL], func=ACT.Sigmoid)
+            nc.scalar.activation(
+                out=gates[bt][:, 2 * CELL : 3 * CELL], in_=gates[bt][:, 2 * CELL : 3 * CELL], func=ACT.Tanh
+            )
+        for bt in tiles:
+            nc.scalar.activation(out=gates[bt][:, 3 * CELL :], in_=gates[bt][:, 3 * CELL :], func=ACT.Sigmoid)
+
+        cells = []
+        cell_moments = []
+        for bt in tiles:
+            kept = stage.tile([P, CELL], F32, tag="kept")
+            nc.vector.tensor_mul(out=kept[:], in0=gates[bt][:, CELL : 2 * CELL], in1=ac_sb[:, bt, :])
+            cell = keep.tile([P, CELL], F32, name="cell_%d" % bt)
+            nc.vector.tensor_mul(out=cell[:], in0=gates[bt][:, :CELL], in1=gates[bt][:, 2 * CELL : 3 * CELL])
+            nc.vector.tensor_add(out=cell[:], in0=cell[:], in1=kept[:])
+            cells.append(cell)
+            cell_moments.append(moments(nc, small, neg_half, cell[:]))
+
+        tanh_acy = []
+        for bt in tiles:
+            mean, rstd = cell_moments[bt]
+            centred = stage.tile([P, CELL], F32, tag="centred_cell")
+            acy = keep.tile([P, CELL], F32, name="acy_%d" % bt)
+            normalise(
+                nc,
+                acy[:],
+                centred[:],
+                cells[bt][:],
+                mean,
+                rstd,
+                spread[:, GAIN_C : GAIN_C + CELL],
+                spread[:, SHIFT_C : SHIFT_C + CELL],
+            )
+            nc.sync.dma_start(out=out_1[bt * P : (bt + 1) * P, :], in_=acy[:])
+            squashed = keep.tile([P, CELL], F32, name="tanh_acy_%d" % bt)
+            nc.scalar.activation(out=squashed[:], in_=acy[:], func=ACT.Tanh)
+            tanh_acy.append(squashed)
+
+        for bt in tiles:
+            ada = keep.tile([P, CELL], F32, name="ada_%d" % bt)
+            nc.vector.tensor_mul(out=ada[:], in0=gates[bt][:, 3 * CELL :], in1=tanh_acy[bt][:])
+            nc.sync.dma_start(out=out_0[bt * P : (bt + 1) * P, :], in_=ada[:])

@@ -142,6 +142,16 @@ def tile_adaptivelstmcell_pa_k_kernel(
         table_warmer = keep.tile([P, 1], F32)
         nc.scalar.activation(out=table_warmer[:], in_=neg_half[:], func=ACT.Sigmoid)
 
+        for quadrant in range(QUADRANTS):
+            for r in range(PLANE_STEP):
+                start = quadrant * QUADRANT + r
+                nc.gpsimd.dma_start(
+                    out=w_planes[start : start + PLANE_PASSES * PLANE_STEP : PLANE_STEP, :, :].bitcast(F32),
+                    in_=a_w_ih_scales[:, quadrant * PLANE_STEP + r, :]
+                    .rearrange("(j i) n -> i j n", i=PLANE_PASSES)
+                    .bitcast(F32),
+                )
+
         ai_tiles = {}
         for chunk in range(CHUNKS):
             source = x if chunk < CHUNKS_IN_X else hx
@@ -151,15 +161,18 @@ def tile_adaptivelstmcell_pa_k_kernel(
                 nc.sync.dma_start(out=ai_tile[:], in_=source[bt * P : (bt + 1) * P, first : first + CHUNK_COLS])
                 ai_tiles[(chunk, bt)] = ai_tile
 
-        for quadrant in range(QUADRANTS):
-            for r in range(PLANE_STEP):
-                start = quadrant * QUADRANT + r
-                nc.sync.dma_start(
-                    out=w_planes[start : start + PLANE_PASSES * PLANE_STEP : PLANE_STEP, :, :].bitcast(I32),
-                    in_=a_w_ih_scales[:, quadrant * PLANE_STEP + r, :]
-                    .rearrange("(j i) n -> i j n", i=PLANE_PASSES)
-                    .bitcast(I32),
-                )
+        ah_sb = keep.tile([P, BATCH_TILES, CELL], BF16)
+        nc.sync.dma_start(out=ah_sb[:], in_=ah.rearrange("(t p) k -> p t k", p=P))
+        whh_sb = keep.tile([P, GATE_COLS // P, CELL], BF16)
+        nc.sync.dma_start(out=whh_sb[:], in_=a_w_hh.rearrange("(c p) k -> p c k", p=P))
+        nc.sync.dma_start(out=rows[0:1, GAIN_H : GAIN_H + GATE_COLS], in_=as_row(a_ln_h_w))
+        nc.sync.dma_start(out=rows[0:1, SHIFT_G : SHIFT_G + GATE_COLS], in_=as_row(a_ln_i_b))
+        nc.sync.dma_start(out=rows[1:2, SHIFT_G : SHIFT_G + GATE_COLS], in_=as_row(a_ln_h_b))
+        nc.sync.dma_start(out=rows[0:1, GAIN_I : GAIN_I + GATE_COLS], in_=as_row(a_ln_i_w))
+        nc.sync.dma_start(out=rows[0:1, GAIN_C : GAIN_C + CELL], in_=as_row(a_ln_c_w))
+        nc.sync.dma_start(out=rows[0:1, SHIFT_C : SHIFT_C + CELL], in_=as_row(a_ln_c_b))
+        ac_sb = keep.tile([P, BATCH_TILES, CELL], BF16)
+        nc.sync.dma_start(out=ac_sb[:], in_=ac.rearrange("(t p) c -> p t c", p=P))
 
         w_tiles = []
         for first_pass in range(0, PASSES, W_LOAD_PASSES):
@@ -171,19 +184,6 @@ def tile_adaptivelstmcell_pa_k_kernel(
                 .bitcast(I32),
             )
             w_tiles.append(w_tile)
-
-        ah_sb = keep.tile([P, BATCH_TILES, CELL], BF16)
-        nc.gpsimd.dma_start(out=ah_sb[:], in_=ah.rearrange("(t p) k -> p t k", p=P))
-        whh_sb = keep.tile([P, GATE_COLS // P, CELL], BF16)
-        nc.gpsimd.dma_start(out=whh_sb[:], in_=a_w_hh.rearrange("(c p) k -> p c k", p=P))
-        nc.gpsimd.dma_start(out=rows[0:1, GAIN_H : GAIN_H + GATE_COLS], in_=as_row(a_ln_h_w))
-        nc.gpsimd.dma_start(out=rows[0:1, SHIFT_G : SHIFT_G + GATE_COLS], in_=as_row(a_ln_i_b))
-        nc.gpsimd.dma_start(out=rows[1:2, SHIFT_G : SHIFT_G + GATE_COLS], in_=as_row(a_ln_h_b))
-        nc.gpsimd.dma_start(out=rows[0:1, GAIN_I : GAIN_I + GATE_COLS], in_=as_row(a_ln_i_w))
-        nc.gpsimd.dma_start(out=rows[0:1, GAIN_C : GAIN_C + CELL], in_=as_row(a_ln_c_w))
-        nc.gpsimd.dma_start(out=rows[0:1, SHIFT_C : SHIFT_C + CELL], in_=as_row(a_ln_c_b))
-        ac_sb = keep.tile([P, BATCH_TILES, CELL], BF16)
-        nc.gpsimd.dma_start(out=ac_sb[:], in_=ac.rearrange("(t p) c -> p t c", p=P))
 
         ai_codes = {}
         ai_scales = {}

@@ -35,7 +35,7 @@ WORDS_PASS = K_PASS // 2
 
 COPY_ROUND = 4
 
-W_LOAD_PASSES = 2
+W_LOAD_PASSES = 1
 
 PLANE_PASSES = 4
 PLANE_STEP = 4
@@ -82,21 +82,29 @@ def regroup_chunk(nc, grouped, filled, first_bank):
             nc.scalar.copy(out=out, in_=in_)
 
 
-def moments(nc, small, neg_half, values):
-    stats = small.tile([P, 6], F32)
-    nc.vector.bn_stats(out=stats[:], in_=values)
-    mean_var = small.tile([P, 2], F32)
-    nc.vector.bn_aggr(out=mean_var[:], in_=stats[:])
-    var_eps = small.tile([P, 1], F32)
-    nc.vector.tensor_scalar_add(out=var_eps[:], in0=mean_var[:, 1:2], scalar1=EPS)
-    rstd = small.tile([P, 1], F32)
+def moments(nc, small, neg_half, values, eps):
+    stats = small.tile([P, BATCH_TILES, 6], F32)
+    for bt in range(BATCH_TILES):
+        nc.vector.bn_stats(out=stats[:, bt, :], in_=values[bt])
+    mean_var = small.tile([P, BATCH_TILES, 2], F32)
+    for bt in range(BATCH_TILES):
+        nc.vector.bn_aggr(out=mean_var[:, bt, :], in_=stats[:, bt, :])
+    var_eps = small.tile([P, BATCH_TILES], F32)
+    nc.vector.tensor_scalar_add(out=var_eps[:], in0=mean_var[:, :, 1], scalar1=eps)
+    rstd = small.tile([P, BATCH_TILES], F32)
     nc.gpsimd.tensor_tensor(out=rstd[:], in0=var_eps[:], in1=neg_half[:], op=ALU.pow)
-    return mean_var[:, 0:1], rstd[:]
+    return mean_var, rstd
 
 
-def normalise(nc, out, centred, values, mean, rstd, gain, shift):
-    nc.vector.scalar_tensor_tensor(out=centred, in0=values, scalar=mean, in1=gain, op0=ALU.subtract, op1=ALU.mult)
-    nc.vector.scalar_tensor_tensor(out=out, in0=centred, scalar=rstd, in1=shift, op0=ALU.mult, op1=ALU.add)
+def normalise(nc, outs, centred, values, mean_var, rstd, gain, shifts):
+    for bt in range(BATCH_TILES):
+        nc.vector.scalar_tensor_tensor(
+            out=centred[:, bt, :], in0=values[bt], scalar=mean_var[:, bt, 0:1], in1=gain, op0=ALU.subtract, op1=ALU.mult
+        )
+    for bt in range(BATCH_TILES):
+        nc.vector.scalar_tensor_tensor(
+            out=outs[bt], in0=centred[:, bt, :], scalar=rstd[:, bt : bt + 1], in1=shifts[bt], op0=ALU.mult, op1=ALU.add
+        )
 
 
 def tile_adaptivelstmcell_pa_k_kernel(
@@ -119,6 +127,8 @@ def tile_adaptivelstmcell_pa_k_kernel(
 ):
     nc = tc.nc
     tiles = range(BATCH_TILES)
+    x_tiles = x.rearrange("(p t) k -> t p k", t=BATCH_TILES)
+    hx_tiles = hx.rearrange("(p t) k -> t p k", t=BATCH_TILES)
     with ExitStack() as ctx:
         ctx.enter_context(tc.manual_schedule())
         keep = ctx.enter_context(tc.tile_pool(name="keep", bufs=1))
@@ -133,46 +143,36 @@ def tile_adaptivelstmcell_pa_k_kernel(
         nc.vector.memset(rows[:], 0.0)
         ones = keep.tile([P, P], BF16)
         nc.vector.memset(ones[:], 1.0)
-        neg_half = keep.tile([P, 1], F32)
+        neg_half = keep.tile([P, BATCH_TILES], F32)
         nc.vector.memset(neg_half[:], -0.5)
         ident_words = keep.tile([P, P], F32)
         masks.make_identity(nc, ident_words[:])
         ident_bf16 = keep.tile([P, P], BF16)
         masks.make_identity(nc, ident_bf16[:])
+        gate_scale = keep.tile([P, GATE_COLS], F32)
+        nc.vector.memset(gate_scale[:], 0.5)
+        nc.vector.memset(gate_scale[:, 2 * CELL : 3 * CELL], 1.0)
         table_warmer = keep.tile([P, 1], F32)
-        nc.scalar.activation(out=table_warmer[:], in_=neg_half[:], func=ACT.Sigmoid)
+        nc.scalar.activation(out=table_warmer[:], in_=neg_half[:, 0:1], func=ACT.Tanh)
+
+        ai_tiles = {}
+        for chunk in range(CHUNKS):
+            source = x_tiles if chunk < CHUNKS_IN_X else hx_tiles
+            first = (chunk % CHUNKS_IN_X) * CHUNK_COLS
+            for bt in tiles:
+                ai_tile = keep.tile([P, CHUNK_COLS], BF16, name="ai_%d_%d" % (chunk, bt))
+                nc.sync.dma_start(out=ai_tile[:], in_=source[bt, :, first : first + CHUNK_COLS])
+                ai_tiles[(chunk, bt)] = ai_tile
 
         for quadrant in range(QUADRANTS):
             for r in range(PLANE_STEP):
                 start = quadrant * QUADRANT + r
-                nc.gpsimd.dma_start(
-                    out=w_planes[start : start + PLANE_PASSES * PLANE_STEP : PLANE_STEP, :, :].bitcast(F32),
+                nc.sync.dma_start(
+                    out=w_planes[start : start + PLANE_PASSES * PLANE_STEP : PLANE_STEP, :, :].bitcast(I32),
                     in_=a_w_ih_scales[:, quadrant * PLANE_STEP + r, :]
                     .rearrange("(j i) n -> i j n", i=PLANE_PASSES)
-                    .bitcast(F32),
+                    .bitcast(I32),
                 )
-
-        ai_tiles = {}
-        for chunk in range(CHUNKS):
-            source = x if chunk < CHUNKS_IN_X else hx
-            first = (chunk % CHUNKS_IN_X) * CHUNK_COLS
-            for bt in tiles:
-                ai_tile = keep.tile([P, CHUNK_COLS], BF16, name="ai_%d_%d" % (chunk, bt))
-                nc.sync.dma_start(out=ai_tile[:], in_=source[bt * P : (bt + 1) * P, first : first + CHUNK_COLS])
-                ai_tiles[(chunk, bt)] = ai_tile
-
-        ah_sb = keep.tile([P, BATCH_TILES, CELL], BF16)
-        nc.sync.dma_start(out=ah_sb[:], in_=ah.rearrange("(t p) k -> p t k", p=P))
-        whh_sb = keep.tile([P, GATE_COLS // P, CELL], BF16)
-        nc.sync.dma_start(out=whh_sb[:], in_=a_w_hh.rearrange("(c p) k -> p c k", p=P))
-        nc.sync.dma_start(out=rows[0:1, GAIN_H : GAIN_H + GATE_COLS], in_=as_row(a_ln_h_w))
-        nc.sync.dma_start(out=rows[0:1, SHIFT_G : SHIFT_G + GATE_COLS], in_=as_row(a_ln_i_b))
-        nc.sync.dma_start(out=rows[1:2, SHIFT_G : SHIFT_G + GATE_COLS], in_=as_row(a_ln_h_b))
-        nc.sync.dma_start(out=rows[0:1, GAIN_I : GAIN_I + GATE_COLS], in_=as_row(a_ln_i_w))
-        nc.sync.dma_start(out=rows[0:1, GAIN_C : GAIN_C + CELL], in_=as_row(a_ln_c_w))
-        nc.sync.dma_start(out=rows[0:1, SHIFT_C : SHIFT_C + CELL], in_=as_row(a_ln_c_b))
-        ac_sb = keep.tile([P, BATCH_TILES, CELL], BF16)
-        nc.sync.dma_start(out=ac_sb[:], in_=ac.rearrange("(t p) c -> p t c", p=P))
 
         w_tiles = []
         for first_pass in range(0, PASSES, W_LOAD_PASSES):
@@ -184,6 +184,19 @@ def tile_adaptivelstmcell_pa_k_kernel(
                 .bitcast(I32),
             )
             w_tiles.append(w_tile)
+
+        ah_sb = keep.tile([P, BATCH_TILES, CELL], BF16)
+        nc.gpsimd.dma_start(out=ah_sb[:], in_=ah.rearrange("(p t) k -> p t k", t=BATCH_TILES))
+        whh_sb = keep.tile([P, GATE_COLS // P, CELL], BF16)
+        nc.gpsimd.dma_start(out=whh_sb[:], in_=a_w_hh.rearrange("(c p) k -> p c k", p=P))
+        nc.gpsimd.dma_start(out=rows[0:1, GAIN_H : GAIN_H + GATE_COLS], in_=as_row(a_ln_h_w))
+        nc.gpsimd.dma_start(out=rows[0:1, SHIFT_G : SHIFT_G + GATE_COLS], in_=as_row(a_ln_i_b))
+        nc.gpsimd.dma_start(out=rows[1:2, SHIFT_G : SHIFT_G + GATE_COLS], in_=as_row(a_ln_h_b))
+        nc.gpsimd.dma_start(out=rows[0:1, GAIN_I : GAIN_I + GATE_COLS], in_=as_row(a_ln_i_w))
+        nc.gpsimd.dma_start(out=rows[0:1, GAIN_C : GAIN_C + CELL], in_=as_row(a_ln_c_w))
+        nc.gpsimd.dma_start(out=rows[0:1, SHIFT_C : SHIFT_C + CELL], in_=as_row(a_ln_c_b))
+        ac_sb = keep.tile([P, BATCH_TILES, CELL], BF16)
+        nc.gpsimd.dma_start(out=ac_sb[:], in_=ac.rearrange("(p t) c -> p t c", t=BATCH_TILES))
 
         ai_codes = {}
         ai_scales = {}
@@ -224,10 +237,12 @@ def tile_adaptivelstmcell_pa_k_kernel(
             nc.tensor.matmul(
                 out=spread_ps[:, :width], lhsT=ones[:], rhs=rows[:, first : first + width], start=True, stop=True
             )
-            nc.scalar.copy(out=spread[:, first : first + width], in_=spread_ps[:, :width])
+            if first < GAIN_C:
+                nc.vector.tensor_mul(out=spread[:, first : first + width], in0=spread_ps[:, :width], in1=gate_scale[:])
+            else:
+                nc.scalar.copy(out=spread[:, first : first + width], in_=spread_ps[:, :width])
 
         hg_ps = []
-        hg_moments = []
         for bt in tiles:
             hg = banks.tile([P, GATE_COLS], F32, tag="bank")
             nc.tensor.matmul(
@@ -237,93 +252,99 @@ def tile_adaptivelstmcell_pa_k_kernel(
                 start=True,
                 stop=True,
             )
-            hg_ps.append(hg)
-            hg_moments.append(moments(nc, small, neg_half, hg[:]))
-        hg_shift = []
-        for bt in tiles:
-            mean, rstd = hg_moments[bt]
-            centred = stage.tile([P, GATE_COLS], F32, tag="centred")
-            shifted = keep.tile([P, GATE_COLS], F32, name="hg_shift_%d" % bt)
-            normalise(
-                nc,
-                shifted[:],
-                centred[:],
-                hg_ps[bt][:],
-                mean,
-                rstd,
-                spread[:, GAIN_H : GAIN_H + GATE_COLS],
-                spread[:, SHIFT_G : SHIFT_G + GATE_COLS],
-            )
-            hg_shift.append(shifted)
+            hg_ps.append(hg[:])
+        mean_var, rstd = moments(nc, small, neg_half, hg_ps, EPS)
+        centred = keep.tile([P, BATCH_TILES, GATE_COLS], F32, tag="centred")
+        hg_shift = keep.tile([P, BATCH_TILES, GATE_COLS], F32)
+        normalise(
+            nc,
+            [hg_shift[:, bt, :] for bt in tiles],
+            centred,
+            hg_ps,
+            mean_var,
+            rstd,
+            spread[:, GAIN_H : GAIN_H + GATE_COLS],
+            [spread[:, SHIFT_G : SHIFT_G + GATE_COLS] for bt in tiles],
+        )
 
         ig_ps = [sums.tile([P, GATE_COLS], F32, name="ig_%d" % bt) for bt in tiles]
-        for g in range(PASSES):
-            w_tile = w_tiles[g // W_LOAD_PASSES]
-            plane_start = (g % PLANE_PASSES) * PLANE_STEP
-            in_chunk = slice((g % CHUNK_PASSES) * P, (g % CHUNK_PASSES + 1) * P)
+        for first_pass in range(0, PASSES, W_LOAD_PASSES):
+            w_tile = w_tiles[first_pass // W_LOAD_PASSES]
             for bt in tiles:
-                key = (g // CHUNK_PASSES, bt)
-                nc.tensor.matmul_mx(
-                    out=ig_ps[bt][:],
-                    lhsT=ai_codes[key][:, in_chunk].bitcast(FP8X4),
-                    lhsT_scale=ai_scales[key][:, in_chunk],
-                    rhs=w_tile[:, g % W_LOAD_PASSES, :].bitcast(FP8X4),
-                    rhs_scale=w_planes[plane_start:P, g // PLANE_PASSES, :],
-                    start=(g == 0),
-                    stop=(g == PASSES - 1),
-                )
+                for g in range(first_pass, first_pass + W_LOAD_PASSES):
+                    key = (g // CHUNK_PASSES, bt)
+                    in_chunk = slice((g % CHUNK_PASSES) * P, (g % CHUNK_PASSES + 1) * P)
+                    nc.tensor.matmul_mx(
+                        out=ig_ps[bt][:],
+                        lhsT=ai_codes[key][:, in_chunk].bitcast(FP8X4),
+                        lhsT_scale=ai_scales[key][:, in_chunk],
+                        rhs=w_tile[:, g - first_pass, :].bitcast(FP8X4),
+                        rhs_scale=w_planes[(g % PLANE_PASSES) * PLANE_STEP : P, g // PLANE_PASSES, :],
+                        start=(g == 0),
+                        stop=(g == PASSES - 1),
+                    )
 
-        ig_moments = [moments(nc, small, neg_half, ig_ps[bt][:]) for bt in tiles]
-        gates = []
+        ig = [ig_ps[bt][:] for bt in tiles]
+        mean_var, rstd = moments(nc, small, neg_half, ig, EPS)
+        centred = keep.tile([P, BATCH_TILES, GATE_COLS], F32, tag="centred")
+        gates = keep.tile([P, BATCH_TILES, GATE_COLS], F32)
+        normalise(
+            nc,
+            [gates[:, bt, :] for bt in tiles],
+            centred,
+            ig,
+            mean_var,
+            rstd,
+            spread[:, GAIN_I : GAIN_I + GATE_COLS],
+            [hg_shift[:, bt, :] for bt in tiles],
+        )
         for bt in tiles:
-            mean, rstd = ig_moments[bt]
-            centred = stage.tile([P, GATE_COLS], F32, tag="centred")
-            g_sum = keep.tile([P, GATE_COLS], F32, name="g_sum_%d" % bt)
-            normalise(
-                nc, g_sum[:], centred[:], ig_ps[bt][:], mean, rstd, spread[:, GAIN_I : GAIN_I + GATE_COLS], hg_shift[bt][:]
+            nc.scalar.activation(out=gates[:, bt, : 3 * CELL], in_=gates[:, bt, : 3 * CELL], func=ACT.Tanh)
+        nc.scalar.activation(out=gates[:, :, 3 * CELL :], in_=gates[:, :, 3 * CELL :], func=ACT.Tanh)
+
+        kept = keep.tile([P, BATCH_TILES, CELL], F32)
+        twice_cell = keep.tile([P, BATCH_TILES, CELL], F32)
+        for bt in tiles:
+            nc.vector.scalar_tensor_tensor(
+                out=kept[:, bt, :],
+                in0=gates[:, bt, 1 * CELL : 2 * CELL],
+                scalar=1.0,
+                in1=ac_sb[:, bt, :],
+                op0=ALU.add,
+                op1=ALU.mult,
             )
-            gates.append(g_sum)
-
-        for bt in tiles:
-            nc.scalar.activation(out=gates[bt][:, : 2 * CELL], in_=gates[bt][:, : 2 * CELL], func=ACT.Sigmoid)
-            nc.scalar.activation(
-                out=gates[bt][:, 2 * CELL : 3 * CELL], in_=gates[bt][:, 2 * CELL : 3 * CELL], func=ACT.Tanh
+            nc.vector.scalar_tensor_tensor(
+                out=twice_cell[:, bt, :],
+                in0=gates[:, bt, 0 * CELL : 1 * CELL],
+                scalar=1.0,
+                in1=gates[:, bt, 2 * CELL : 3 * CELL],
+                op0=ALU.add,
+                op1=ALU.mult,
             )
-        for bt in tiles:
-            nc.scalar.activation(out=gates[bt][:, 3 * CELL :], in_=gates[bt][:, 3 * CELL :], func=ACT.Sigmoid)
+        nc.vector.tensor_add(out=twice_cell[:], in0=twice_cell[:], in1=kept[:])
+        cells = [twice_cell[:, bt, :] for bt in tiles]
+        mean_var, rstd = moments(nc, small, neg_half, cells, 4.0 * EPS)
 
-        cells = []
-        cell_moments = []
-        for bt in tiles:
-            kept = stage.tile([P, CELL], F32, tag="kept")
-            nc.vector.tensor_mul(out=kept[:], in0=gates[bt][:, CELL : 2 * CELL], in1=ac_sb[:, bt, :])
-            cell = keep.tile([P, CELL], F32, name="cell_%d" % bt)
-            nc.vector.tensor_mul(out=cell[:], in0=gates[bt][:, :CELL], in1=gates[bt][:, 2 * CELL : 3 * CELL])
-            nc.vector.tensor_add(out=cell[:], in0=cell[:], in1=kept[:])
-            cells.append(cell)
-            cell_moments.append(moments(nc, small, neg_half, cell[:]))
+        sigmoid_o = keep.tile([P, BATCH_TILES, CELL], F32)
+        nc.vector.tensor_scalar(
+            out=sigmoid_o[:], in0=gates[:, :, 3 * CELL :], scalar1=0.5, scalar2=0.5, op0=ALU.mult, op1=ALU.add
+        )
 
-        tanh_acy = []
-        for bt in tiles:
-            mean, rstd = cell_moments[bt]
-            centred = stage.tile([P, CELL], F32, tag="centred_cell")
-            acy = keep.tile([P, CELL], F32, name="acy_%d" % bt)
-            normalise(
-                nc,
-                acy[:],
-                centred[:],
-                cells[bt][:],
-                mean,
-                rstd,
-                spread[:, GAIN_C : GAIN_C + CELL],
-                spread[:, SHIFT_C : SHIFT_C + CELL],
-            )
-            nc.sync.dma_start(out=out_1[bt * P : (bt + 1) * P, :], in_=acy[:])
-            squashed = keep.tile([P, CELL], F32, name="tanh_acy_%d" % bt)
-            nc.scalar.activation(out=squashed[:], in_=acy[:], func=ACT.Tanh)
-            tanh_acy.append(squashed)
-
-        for bt in tiles:
-            ada = keep.tile([P, CELL], F32, name="ada_%d" % bt)
-            nc.vector.tensor_mul(out=ada[:], in0=gates[bt][:, 3 * CELL :], in1=tanh_acy[bt][:])
-            nc.sync.dma_start(out=out_0[bt * P : (bt + 1) * P, :], in_=ada[:])
+        centred_cell = keep.tile([P, BATCH_TILES, CELL], F32)
+        acy = keep.tile([P, BATCH_TILES, CELL], F32)
+        normalise(
+            nc,
+            [acy[:, bt, :] for bt in tiles],
+            centred_cell,
+            cells,
+            mean_var,
+            rstd,
+            spread[:, GAIN_C : GAIN_C + CELL],
+            [spread[:, SHIFT_C : SHIFT_C + CELL] for bt in tiles],
+        )
+        nc.sync.dma_start(out=out_1.rearrange("(p t) c -> p t c", t=BATCH_TILES), in_=acy[:])
+        tanh_acy = keep.tile([P, BATCH_TILES, CELL], F32)
+        nc.scalar.activation(out=tanh_acy[:], in_=acy[:], func=ACT.Tanh)
+        ada = keep.tile([P, BATCH_TILES, CELL], F32)
+        nc.vector.tensor_mul(out=ada[:], in0=sigmoid_o[:], in1=tanh_acy[:])
+        nc.sync.dma_start(out=out_0.rearrange("(p t) c -> p t c", t=BATCH_TILES), in_=ada[:])

@@ -23,6 +23,7 @@ PASSES = K // K_PASS
 GATE_COLS = 512
 CELL = 128
 EPS = 1e-5
+PLAIN_AFTER = 20
 
 FLOPS = 2 * BATCH * K * GATE_COLS + 2 * BATCH * CELL * GATE_COLS
 
@@ -147,6 +148,16 @@ def tile_adaptivelstmcell_pa_k_kernel(
         nc.vector.memset(neg_half[:], -0.5)
         ident_words = keep.tile([P, P], F32)
         masks.make_identity(nc, ident_words[:])
+        for quadrant in range(QUADRANTS):
+            for r in range(PLANE_STEP):
+                start = quadrant * QUADRANT + r
+                nc.gpsimd.dma_start(
+                    out=w_planes[start : start + PLANE_PASSES * PLANE_STEP : PLANE_STEP, :, :].bitcast(I32),
+                    in_=a_w_ih_scales[:, quadrant * PLANE_STEP + r, :]
+                    .rearrange("(j i) n -> i j n", i=PLANE_PASSES)
+                    .bitcast(I32),
+                )
+
         ident_bf16 = keep.tile([P, P], BF16)
         masks.make_identity(nc, ident_bf16[:])
         gate_scale = keep.tile([P, GATE_COLS], F32)
@@ -163,16 +174,6 @@ def tile_adaptivelstmcell_pa_k_kernel(
                 ai_tile = keep.tile([P, CHUNK_COLS], BF16, name="ai_%d_%d" % (chunk, bt))
                 nc.sync.dma_start(out=ai_tile[:], in_=source[bt, :, first : first + CHUNK_COLS])
                 ai_tiles[(chunk, bt)] = ai_tile
-
-        for quadrant in range(QUADRANTS):
-            for r in range(PLANE_STEP):
-                start = quadrant * QUADRANT + r
-                nc.sync.dma_start(
-                    out=w_planes[start : start + PLANE_PASSES * PLANE_STEP : PLANE_STEP, :, :].bitcast(I32),
-                    in_=a_w_ih_scales[:, quadrant * PLANE_STEP + r, :]
-                    .rearrange("(j i) n -> i j n", i=PLANE_PASSES)
-                    .bitcast(I32),
-                )
 
         w_tiles = []
         for first_pass in range(0, PASSES, W_LOAD_PASSES):
@@ -222,53 +223,57 @@ def tile_adaptivelstmcell_pa_k_kernel(
             regrouped = (key, grouped)
         quantise_chunk(regrouped[0], regrouped[1])
 
-        k_first_ps = banks.tile([P, BATCH_TILES + GATE_COLS // P, P], BF16, tag="bank")
-        for bt in tiles:
-            nc.tensor.transpose(out=k_first_ps[:, bt, :], in_=ah_sb[:, bt, :], identity=ident_bf16[:])
-        for c in range(GATE_COLS // P):
-            nc.tensor.transpose(out=k_first_ps[:, BATCH_TILES + c, :], in_=whh_sb[:, c, :], identity=ident_bf16[:])
-        k_first = keep.tile([P, BATCH_TILES + GATE_COLS // P, P], BF16)
-        nc.scalar.copy(out=k_first[:], in_=k_first_ps[:])
+        def plain_work():
+            k_first_ps = banks.tile([P, BATCH_TILES + GATE_COLS // P, P], BF16, tag="bank")
+            for bt in tiles:
+                nc.tensor.transpose(out=k_first_ps[:, bt, :], in_=ah_sb[:, bt, :], identity=ident_bf16[:])
+            for c in range(GATE_COLS // P):
+                nc.tensor.transpose(out=k_first_ps[:, BATCH_TILES + c, :], in_=whh_sb[:, c, :], identity=ident_bf16[:])
+            k_first = keep.tile([P, BATCH_TILES + GATE_COLS // P, P], BF16)
+            nc.scalar.copy(out=k_first[:], in_=k_first_ps[:])
 
-        spread = keep.tile([P, ROW_COLS], F32)
-        for first in range(0, ROW_COLS, GATE_COLS):
-            width = min(GATE_COLS, ROW_COLS - first)
-            spread_ps = banks.tile([P, GATE_COLS], F32, tag="bank")
-            nc.tensor.matmul(
-                out=spread_ps[:, :width], lhsT=ones[:], rhs=rows[:, first : first + width], start=True, stop=True
-            )
-            if first < GAIN_C:
-                nc.vector.tensor_mul(out=spread[:, first : first + width], in0=spread_ps[:, :width], in1=gate_scale[:])
-            else:
-                nc.scalar.copy(out=spread[:, first : first + width], in_=spread_ps[:, :width])
+            spread = keep.tile([P, ROW_COLS], F32)
+            for first in range(0, ROW_COLS, GATE_COLS):
+                width = min(GATE_COLS, ROW_COLS - first)
+                spread_ps = banks.tile([P, GATE_COLS], F32, tag="bank")
+                nc.tensor.matmul(
+                    out=spread_ps[:, :width], lhsT=ones[:], rhs=rows[:, first : first + width], start=True, stop=True
+                )
+                if first < GAIN_C:
+                    nc.vector.tensor_mul(out=spread[:, first : first + width], in0=spread_ps[:, :width], in1=gate_scale[:])
+                else:
+                    nc.scalar.copy(out=spread[:, first : first + width], in_=spread_ps[:, :width])
 
-        hg_ps = []
-        for bt in tiles:
-            hg = banks.tile([P, GATE_COLS], F32, tag="bank")
-            nc.tensor.matmul(
-                out=hg[:],
-                lhsT=k_first[:, bt, :],
-                rhs=k_first[:, BATCH_TILES:, :].rearrange("p c n -> p (c n)"),
-                start=True,
-                stop=True,
+            hg_ps = []
+            for bt in tiles:
+                hg = banks.tile([P, GATE_COLS], F32, tag="bank")
+                nc.tensor.matmul(
+                    out=hg[:],
+                    lhsT=k_first[:, bt, :],
+                    rhs=k_first[:, BATCH_TILES:, :].rearrange("p c n -> p (c n)"),
+                    start=True,
+                    stop=True,
+                )
+                hg_ps.append(hg[:])
+            mean_var, rstd = moments(nc, small, neg_half, hg_ps, EPS)
+            centred = keep.tile([P, BATCH_TILES, GATE_COLS], F32, tag="centred")
+            hg_shift = keep.tile([P, BATCH_TILES, GATE_COLS], F32)
+            normalise(
+                nc,
+                [hg_shift[:, bt, :] for bt in tiles],
+                centred,
+                hg_ps,
+                mean_var,
+                rstd,
+                spread[:, GAIN_H : GAIN_H + GATE_COLS],
+                [spread[:, SHIFT_G : SHIFT_G + GATE_COLS] for bt in tiles],
             )
-            hg_ps.append(hg[:])
-        mean_var, rstd = moments(nc, small, neg_half, hg_ps, EPS)
-        centred = keep.tile([P, BATCH_TILES, GATE_COLS], F32, tag="centred")
-        hg_shift = keep.tile([P, BATCH_TILES, GATE_COLS], F32)
-        normalise(
-            nc,
-            [hg_shift[:, bt, :] for bt in tiles],
-            centred,
-            hg_ps,
-            mean_var,
-            rstd,
-            spread[:, GAIN_H : GAIN_H + GATE_COLS],
-            [spread[:, SHIFT_G : SHIFT_G + GATE_COLS] for bt in tiles],
-        )
+            return hg_shift, spread
 
         ig_ps = [sums.tile([P, GATE_COLS], F32, name="ig_%d" % bt) for bt in tiles]
         for first_pass in range(0, PASSES, W_LOAD_PASSES):
+            if first_pass == PLAIN_AFTER:
+                hg_shift, spread = plain_work()
             w_tile = w_tiles[first_pass // W_LOAD_PASSES]
             for bt in tiles:
                 for g in range(first_pass, first_pass + W_LOAD_PASSES):

@@ -23,7 +23,6 @@ PASSES = K // K_PASS
 GATE_COLS = 512
 CELL = 128
 EPS = 1e-5
-PLAIN_AFTER = 20
 
 FLOPS = 2 * BATCH * K * GATE_COLS + 2 * BATCH * CELL * GATE_COLS
 
@@ -36,12 +35,15 @@ WORDS_PASS = K_PASS // 2
 
 COPY_ROUND = 4
 
-W_LOAD_PASSES = 1
+W_LOADS = (2,) * 14 + (1,) * 4
 
-PLANE_PASSES = 4
+TILE_PASSES = 8
 PLANE_STEP = 4
 QUADRANTS = 4
 QUADRANT = P // QUADRANTS
+
+TURN_PASS = 2
+HIDDEN_PASS = 6
 
 GAIN_I = 0
 GAIN_H = GAIN_I + GATE_COLS
@@ -138,34 +140,56 @@ def tile_adaptivelstmcell_pa_k_kernel(
         banks = ctx.enter_context(tc.psum_pool(name="banks", bufs=6))
         sums = ctx.enter_context(tc.psum_pool(name="sums", bufs=1))
 
-        w_planes = keep.tile([P, PASSES // PLANE_PASSES, GATE_COLS], U8, align_bytes=64)
-        nc.vector.memset(w_planes[:].bitcast(I32), 0)
+        neg_half = keep.tile([P, BATCH_TILES], F32)
+        nc.vector.memset(neg_half[:], -0.5)
+        w_planes = []
+
+        def load_scales(i):
+            planes = keep.tile([P, TILE_PASSES, GATE_COLS], U8, name="planes_%d" % i, align_bytes=64)
+            nc.vector.memset(planes[:].bitcast(I32), 0)
+            for quadrant in range(QUADRANTS):
+                start = quadrant * QUADRANT + i * PLANE_STEP
+                nc.gpsimd.dma_start(
+                    out=planes[start : start + PLANE_STEP, :, :].bitcast(I32),
+                    in_=a_w_ih_scales[
+                        i * TILE_PASSES : (i + 1) * TILE_PASSES,
+                        quadrant * PLANE_STEP : (quadrant + 1) * PLANE_STEP,
+                        :,
+                    ]
+                    .rearrange("j r n -> r j n")
+                    .bitcast(I32),
+                )
+            w_planes.append(planes)
+
         rows = keep.tile([P, ROW_COLS], BF16)
         nc.vector.memset(rows[:], 0.0)
         ones = keep.tile([P, P], BF16)
         nc.vector.memset(ones[:], 1.0)
-        neg_half = keep.tile([P, BATCH_TILES], F32)
-        nc.vector.memset(neg_half[:], -0.5)
         ident_words = keep.tile([P, P], F32)
         masks.make_identity(nc, ident_words[:])
-        for quadrant in range(QUADRANTS):
-            for r in range(PLANE_STEP):
-                start = quadrant * QUADRANT + r
-                nc.gpsimd.dma_start(
-                    out=w_planes[start : start + PLANE_PASSES * PLANE_STEP : PLANE_STEP, :, :].bitcast(I32),
-                    in_=a_w_ih_scales[:, quadrant * PLANE_STEP + r, :]
-                    .rearrange("(j i) n -> i j n", i=PLANE_PASSES)
-                    .bitcast(I32),
-                )
-
         ident_bf16 = keep.tile([P, P], BF16)
-        masks.make_identity(nc, ident_bf16[:])
+        nc.scalar.copy(out=ident_bf16[:], in_=ident_words[:])
+        load_scales(0)
         gate_scale = keep.tile([P, GATE_COLS], F32)
         nc.vector.memset(gate_scale[:], 0.5)
         nc.vector.memset(gate_scale[:, 2 * CELL : 3 * CELL], 1.0)
         table_warmer = keep.tile([P, 1], F32)
         nc.scalar.activation(out=table_warmer[:], in_=neg_half[:, 0:1], func=ACT.Tanh)
 
+        ah_sb = keep.tile([P, BATCH_TILES, CELL], BF16)
+        whh_sb = keep.tile([P, GATE_COLS // P, CELL], BF16)
+        ac_sb = keep.tile([P, BATCH_TILES, CELL], BF16)
+        small_loads = [
+            (ah_sb[:], ah.rearrange("(p t) k -> p t k", t=BATCH_TILES)),
+            (whh_sb[:], a_w_hh.rearrange("(c p) k -> p c k", p=P)),
+            (rows[0:1, GAIN_H : GAIN_H + GATE_COLS], as_row(a_ln_h_w)),
+            (rows[0:1, SHIFT_G : SHIFT_G + GATE_COLS], as_row(a_ln_i_b)),
+            (rows[1:2, SHIFT_G : SHIFT_G + GATE_COLS], as_row(a_ln_h_b)),
+            (rows[0:1, GAIN_I : GAIN_I + GATE_COLS], as_row(a_ln_i_w)),
+            (rows[0:1, GAIN_C : GAIN_C + CELL], as_row(a_ln_c_w)),
+            (rows[0:1, SHIFT_C : SHIFT_C + CELL], as_row(a_ln_c_b)),
+            (ac_sb[:], ac.rearrange("(p t) c -> p t c", t=BATCH_TILES)),
+        ]
         ai_tiles = {}
         for chunk in range(CHUNKS):
             source = x_tiles if chunk < CHUNKS_IN_X else hx_tiles
@@ -174,30 +198,22 @@ def tile_adaptivelstmcell_pa_k_kernel(
                 ai_tile = keep.tile([P, CHUNK_COLS], BF16, name="ai_%d_%d" % (chunk, bt))
                 nc.sync.dma_start(out=ai_tile[:], in_=source[bt, :, first : first + CHUNK_COLS])
                 ai_tiles[(chunk, bt)] = ai_tile
+                small_load = chunk * BATCH_TILES + bt - BATCH_TILES
+                if 0 <= small_load < len(small_loads):
+                    out, in_ = small_loads[small_load]
+                    nc.sync.dma_start(out=out, in_=in_)
 
-        w_tiles = []
-        for first_pass in range(0, PASSES, W_LOAD_PASSES):
-            w_tile = keep.tile([P, W_LOAD_PASSES, GATE_COLS], U32, name="w_%d" % first_pass, align_bytes=64)
+        w_tiles = {}
+        first_pass = 0
+        for passes in W_LOADS:
+            w_tile = keep.tile([P, passes, GATE_COLS], U32, name="w_%d" % first_pass, align_bytes=64)
             nc.sync.dma_start(
                 out=w_tile[:].bitcast(I32),
-                in_=a_w_ih_words[first_pass : first_pass + W_LOAD_PASSES]
-                .rearrange("g p n t -> p g (n t)")
-                .bitcast(I32),
+                in_=a_w_ih_words[first_pass : first_pass + passes].rearrange("g p n t -> p g (n t)").bitcast(I32),
             )
-            w_tiles.append(w_tile)
-
-        ah_sb = keep.tile([P, BATCH_TILES, CELL], BF16)
-        nc.gpsimd.dma_start(out=ah_sb[:], in_=ah.rearrange("(p t) k -> p t k", t=BATCH_TILES))
-        whh_sb = keep.tile([P, GATE_COLS // P, CELL], BF16)
-        nc.gpsimd.dma_start(out=whh_sb[:], in_=a_w_hh.rearrange("(c p) k -> p c k", p=P))
-        nc.gpsimd.dma_start(out=rows[0:1, GAIN_H : GAIN_H + GATE_COLS], in_=as_row(a_ln_h_w))
-        nc.gpsimd.dma_start(out=rows[0:1, SHIFT_G : SHIFT_G + GATE_COLS], in_=as_row(a_ln_i_b))
-        nc.gpsimd.dma_start(out=rows[1:2, SHIFT_G : SHIFT_G + GATE_COLS], in_=as_row(a_ln_h_b))
-        nc.gpsimd.dma_start(out=rows[0:1, GAIN_I : GAIN_I + GATE_COLS], in_=as_row(a_ln_i_w))
-        nc.gpsimd.dma_start(out=rows[0:1, GAIN_C : GAIN_C + CELL], in_=as_row(a_ln_c_w))
-        nc.gpsimd.dma_start(out=rows[0:1, SHIFT_C : SHIFT_C + CELL], in_=as_row(a_ln_c_b))
-        ac_sb = keep.tile([P, BATCH_TILES, CELL], BF16)
-        nc.gpsimd.dma_start(out=ac_sb[:], in_=ac.rearrange("(p t) c -> p t c", t=BATCH_TILES))
+            for i in range(passes):
+                w_tiles[first_pass + i] = (w_tile, i)
+            first_pass += passes
 
         ai_codes = {}
         ai_scales = {}
@@ -221,9 +237,13 @@ def tile_adaptivelstmcell_pa_k_kernel(
             grouped = stage.tile([P, CHUNK_PASSES, P, PACK], BF16, align_bytes=64)
             regroup_chunk(nc, grouped, filled, step * len(filled))
             regrouped = (key, grouped)
+            if step + 1 < PASSES // TILE_PASSES:
+                load_scales(step + 1)
         quantise_chunk(regrouped[0], regrouped[1])
 
-        def plain_work():
+        gates = keep.tile([P, BATCH_TILES, GATE_COLS + CELL], F32)
+
+        def turn_small():
             k_first_ps = banks.tile([P, BATCH_TILES + GATE_COLS // P, P], BF16, tag="bank")
             for bt in tiles:
                 nc.tensor.transpose(out=k_first_ps[:, bt, :], in_=ah_sb[:, bt, :], identity=ident_bf16[:])
@@ -231,6 +251,7 @@ def tile_adaptivelstmcell_pa_k_kernel(
                 nc.tensor.transpose(out=k_first_ps[:, BATCH_TILES + c, :], in_=whh_sb[:, c, :], identity=ident_bf16[:])
             k_first = keep.tile([P, BATCH_TILES + GATE_COLS // P, P], BF16)
             nc.scalar.copy(out=k_first[:], in_=k_first_ps[:])
+            nc.scalar.copy(out=gates[:, :, 3 * CELL : 4 * CELL], in_=ac_sb[:])
 
             spread = keep.tile([P, ROW_COLS], F32)
             for first in range(0, ROW_COLS, GATE_COLS):
@@ -243,7 +264,9 @@ def tile_adaptivelstmcell_pa_k_kernel(
                     nc.vector.tensor_mul(out=spread[:, first : first + width], in0=spread_ps[:, :width], in1=gate_scale[:])
                 else:
                     nc.scalar.copy(out=spread[:, first : first + width], in_=spread_ps[:, :width])
+            return k_first, spread
 
+        def hidden_gates():
             hg_ps = []
             for bt in tiles:
                 hg = banks.tile([P, GATE_COLS], F32, tag="bank")
@@ -268,71 +291,76 @@ def tile_adaptivelstmcell_pa_k_kernel(
                 spread[:, GAIN_H : GAIN_H + GATE_COLS],
                 [spread[:, SHIFT_G : SHIFT_G + GATE_COLS] for bt in tiles],
             )
-            return hg_shift, spread
+            return hg_shift
 
         ig_ps = [sums.tile([P, GATE_COLS], F32, name="ig_%d" % bt) for bt in tiles]
-        for first_pass in range(0, PASSES, W_LOAD_PASSES):
-            if first_pass == PLAIN_AFTER:
-                hg_shift, spread = plain_work()
-            w_tile = w_tiles[first_pass // W_LOAD_PASSES]
+        for g in range(PASSES):
+            if g == TURN_PASS:
+                k_first, spread = turn_small()
+            if g == HIDDEN_PASS:
+                hg_shift = hidden_gates()
+            w_tile, index = w_tiles[g]
+            in_chunk = slice((g % CHUNK_PASSES) * P, (g % CHUNK_PASSES + 1) * P)
             for bt in tiles:
-                for g in range(first_pass, first_pass + W_LOAD_PASSES):
-                    key = (g // CHUNK_PASSES, bt)
-                    in_chunk = slice((g % CHUNK_PASSES) * P, (g % CHUNK_PASSES + 1) * P)
-                    nc.tensor.matmul_mx(
-                        out=ig_ps[bt][:],
-                        lhsT=ai_codes[key][:, in_chunk].bitcast(FP8X4),
-                        lhsT_scale=ai_scales[key][:, in_chunk],
-                        rhs=w_tile[:, g - first_pass, :].bitcast(FP8X4),
-                        rhs_scale=w_planes[(g % PLANE_PASSES) * PLANE_STEP : P, g // PLANE_PASSES, :],
-                        start=(g == 0),
-                        stop=(g == PASSES - 1),
-                    )
+                key = (g // CHUNK_PASSES, bt)
+                nc.tensor.matmul_mx(
+                    out=ig_ps[bt][:],
+                    lhsT=ai_codes[key][:, in_chunk].bitcast(FP8X4),
+                    lhsT_scale=ai_scales[key][:, in_chunk],
+                    rhs=w_tile[:, index, :].bitcast(FP8X4),
+                    rhs_scale=w_planes[g // TILE_PASSES][(g // TILE_PASSES) * PLANE_STEP : P, g % TILE_PASSES, :],
+                    start=(g == 0),
+                    stop=(g == PASSES - 1),
+                )
 
         ig = [ig_ps[bt][:] for bt in tiles]
         mean_var, rstd = moments(nc, small, neg_half, ig, EPS)
         centred = keep.tile([P, BATCH_TILES, GATE_COLS], F32, tag="centred")
-        gates = keep.tile([P, BATCH_TILES, GATE_COLS], F32)
-        normalise(
-            nc,
-            [gates[:, bt, :] for bt in tiles],
-            centred,
-            ig,
-            mean_var,
-            rstd,
-            spread[:, GAIN_I : GAIN_I + GATE_COLS],
-            [hg_shift[:, bt, :] for bt in tiles],
-        )
+        for part in (slice(0, 3 * CELL), slice(3 * CELL, GATE_COLS)):
+            for bt in tiles:
+                nc.vector.scalar_tensor_tensor(
+                    out=centred[:, bt, part],
+                    in0=ig[bt][:, part],
+                    scalar=mean_var[:, bt, 0:1],
+                    in1=spread[:, GAIN_I + part.start : GAIN_I + part.stop],
+                    op0=ALU.subtract,
+                    op1=ALU.mult,
+                )
+        for part, first in ((slice(0, 3 * CELL), 0), (slice(3 * CELL, GATE_COLS), 4 * CELL)):
+            for bt in tiles:
+                nc.vector.scalar_tensor_tensor(
+                    out=gates[:, bt, first : first + part.stop - part.start],
+                    in0=centred[:, bt, part],
+                    scalar=rstd[:, bt : bt + 1],
+                    in1=hg_shift[:, bt, part],
+                    op0=ALU.mult,
+                    op1=ALU.add,
+                )
         for bt in tiles:
             nc.scalar.activation(out=gates[:, bt, : 3 * CELL], in_=gates[:, bt, : 3 * CELL], func=ACT.Tanh)
-        nc.scalar.activation(out=gates[:, :, 3 * CELL :], in_=gates[:, :, 3 * CELL :], func=ACT.Tanh)
+        nc.scalar.activation(out=gates[:, :, 4 * CELL :], in_=gates[:, :, 4 * CELL :], func=ACT.Tanh)
 
-        kept = keep.tile([P, BATCH_TILES, CELL], F32)
+        products = keep.tile([P, BATCH_TILES, 2 * CELL], F32)
         twice_cell = keep.tile([P, BATCH_TILES, CELL], F32)
         for bt in tiles:
             nc.vector.scalar_tensor_tensor(
-                out=kept[:, bt, :],
-                in0=gates[:, bt, 1 * CELL : 2 * CELL],
+                out=products[:, bt, :],
+                in0=gates[:, bt, : 2 * CELL],
                 scalar=1.0,
-                in1=ac_sb[:, bt, :],
+                in1=gates[:, bt, 2 * CELL : 4 * CELL],
                 op0=ALU.add,
                 op1=ALU.mult,
             )
-            nc.vector.scalar_tensor_tensor(
-                out=twice_cell[:, bt, :],
-                in0=gates[:, bt, 0 * CELL : 1 * CELL],
-                scalar=1.0,
-                in1=gates[:, bt, 2 * CELL : 3 * CELL],
-                op0=ALU.add,
-                op1=ALU.mult,
+        for bt in tiles:
+            nc.vector.tensor_add(
+                out=twice_cell[:, bt, :], in0=products[:, bt, :CELL], in1=products[:, bt, CELL:]
             )
-        nc.vector.tensor_add(out=twice_cell[:], in0=twice_cell[:], in1=kept[:])
         cells = [twice_cell[:, bt, :] for bt in tiles]
         mean_var, rstd = moments(nc, small, neg_half, cells, 4.0 * EPS)
 
         sigmoid_o = keep.tile([P, BATCH_TILES, CELL], F32)
         nc.vector.tensor_scalar(
-            out=sigmoid_o[:], in0=gates[:, :, 3 * CELL :], scalar1=0.5, scalar2=0.5, op0=ALU.mult, op1=ALU.add
+            out=sigmoid_o[:], in0=gates[:, :, 4 * CELL :], scalar1=0.5, scalar2=0.5, op0=ALU.mult, op1=ALU.add
         )
 
         centred_cell = keep.tile([P, BATCH_TILES, CELL], F32)
@@ -349,7 +377,9 @@ def tile_adaptivelstmcell_pa_k_kernel(
         )
         nc.sync.dma_start(out=out_1.rearrange("(p t) c -> p t c", t=BATCH_TILES), in_=acy[:])
         tanh_acy = keep.tile([P, BATCH_TILES, CELL], F32)
-        nc.scalar.activation(out=tanh_acy[:], in_=acy[:], func=ACT.Tanh)
         ada = keep.tile([P, BATCH_TILES, CELL], F32)
-        nc.vector.tensor_mul(out=ada[:], in0=sigmoid_o[:], in1=tanh_acy[:])
+        for bt in tiles:
+            nc.scalar.activation(out=tanh_acy[:, bt, :], in_=acy[:, bt, :], func=ACT.Tanh)
+        for bt in tiles:
+            nc.vector.tensor_mul(out=ada[:, bt, :], in0=sigmoid_o[:, bt, :], in1=tanh_acy[:, bt, :])
         nc.sync.dma_start(out=out_0.rearrange("(p t) c -> p t c", t=BATCH_TILES), in_=ada[:])

@@ -35,9 +35,9 @@ WORDS_PASS = K_PASS // 2
 
 COPY_ROUND = 4
 
-W_LOADS = (2,) * 14 + (1,) * 4
+W_LOADS = (1,) * PASSES
 
-TILE_PASSES = 8
+PLANE_PASSES = 4
 PLANE_STEP = 4
 QUADRANTS = 4
 QUADRANT = P // QUADRANTS
@@ -142,25 +142,8 @@ def tile_adaptivelstmcell_pa_k_kernel(
 
         neg_half = keep.tile([P, BATCH_TILES], F32)
         nc.vector.memset(neg_half[:], -0.5)
-        w_planes = []
-
-        def load_scales(i):
-            planes = keep.tile([P, TILE_PASSES, GATE_COLS], U8, name="planes_%d" % i, align_bytes=64)
-            nc.vector.memset(planes[:].bitcast(I32), 0)
-            for quadrant in range(QUADRANTS):
-                start = quadrant * QUADRANT + i * PLANE_STEP
-                nc.gpsimd.dma_start(
-                    out=planes[start : start + PLANE_STEP, :, :].bitcast(I32),
-                    in_=a_w_ih_scales[
-                        i * TILE_PASSES : (i + 1) * TILE_PASSES,
-                        quadrant * PLANE_STEP : (quadrant + 1) * PLANE_STEP,
-                        :,
-                    ]
-                    .rearrange("j r n -> r j n")
-                    .bitcast(I32),
-                )
-            w_planes.append(planes)
-
+        w_planes = keep.tile([P, PASSES // PLANE_PASSES, GATE_COLS], U8, align_bytes=64)
+        nc.vector.memset(w_planes[:].bitcast(I32), 0)
         rows = keep.tile([P, ROW_COLS], BF16)
         nc.vector.memset(rows[:], 0.0)
         ones = keep.tile([P, P], BF16)
@@ -169,27 +152,22 @@ def tile_adaptivelstmcell_pa_k_kernel(
         masks.make_identity(nc, ident_words[:])
         ident_bf16 = keep.tile([P, P], BF16)
         nc.scalar.copy(out=ident_bf16[:], in_=ident_words[:])
-        load_scales(0)
         gate_scale = keep.tile([P, GATE_COLS], F32)
         nc.vector.memset(gate_scale[:], 0.5)
         nc.vector.memset(gate_scale[:, 2 * CELL : 3 * CELL], 1.0)
         table_warmer = keep.tile([P, 1], F32)
         nc.scalar.activation(out=table_warmer[:], in_=neg_half[:, 0:1], func=ACT.Tanh)
 
-        ah_sb = keep.tile([P, BATCH_TILES, CELL], BF16)
-        whh_sb = keep.tile([P, GATE_COLS // P, CELL], BF16)
-        ac_sb = keep.tile([P, BATCH_TILES, CELL], BF16)
-        small_loads = [
-            (ah_sb[:], ah.rearrange("(p t) k -> p t k", t=BATCH_TILES)),
-            (whh_sb[:], a_w_hh.rearrange("(c p) k -> p c k", p=P)),
-            (rows[0:1, GAIN_H : GAIN_H + GATE_COLS], as_row(a_ln_h_w)),
-            (rows[0:1, SHIFT_G : SHIFT_G + GATE_COLS], as_row(a_ln_i_b)),
-            (rows[1:2, SHIFT_G : SHIFT_G + GATE_COLS], as_row(a_ln_h_b)),
-            (rows[0:1, GAIN_I : GAIN_I + GATE_COLS], as_row(a_ln_i_w)),
-            (rows[0:1, GAIN_C : GAIN_C + CELL], as_row(a_ln_c_w)),
-            (rows[0:1, SHIFT_C : SHIFT_C + CELL], as_row(a_ln_c_b)),
-            (ac_sb[:], ac.rearrange("(p t) c -> p t c", t=BATCH_TILES)),
-        ]
+        def load_scales(quadrant, r):
+            start = quadrant * QUADRANT + r
+            nc.sync.dma_start(
+                out=w_planes[start : start + PLANE_PASSES * PLANE_STEP : PLANE_STEP, :, :].bitcast(I32),
+                in_=a_w_ih_scales[:, quadrant * PLANE_STEP + r, :]
+                .rearrange("(j i) n -> i j n", i=PLANE_PASSES)
+                .bitcast(I32),
+            )
+
+        scale_loads = [(quadrant, r) for quadrant in range(QUADRANTS) for r in range(PLANE_STEP)]
         ai_tiles = {}
         for chunk in range(CHUNKS):
             source = x_tiles if chunk < CHUNKS_IN_X else hx_tiles
@@ -198,10 +176,20 @@ def tile_adaptivelstmcell_pa_k_kernel(
                 ai_tile = keep.tile([P, CHUNK_COLS], BF16, name="ai_%d_%d" % (chunk, bt))
                 nc.sync.dma_start(out=ai_tile[:], in_=source[bt, :, first : first + CHUNK_COLS])
                 ai_tiles[(chunk, bt)] = ai_tile
-                small_load = chunk * BATCH_TILES + bt - BATCH_TILES
-                if 0 <= small_load < len(small_loads):
-                    out, in_ = small_loads[small_load]
-                    nc.sync.dma_start(out=out, in_=in_)
+                load_scales(*scale_loads[chunk * BATCH_TILES + bt])
+
+        ah_sb = keep.tile([P, BATCH_TILES, CELL], BF16)
+        nc.gpsimd.dma_start(out=ah_sb[:], in_=ah.rearrange("(p t) k -> p t k", t=BATCH_TILES))
+        whh_sb = keep.tile([P, GATE_COLS // P, CELL], BF16)
+        nc.gpsimd.dma_start(out=whh_sb[:], in_=a_w_hh.rearrange("(c p) k -> p c k", p=P))
+        nc.gpsimd.dma_start(out=rows[0:1, GAIN_H : GAIN_H + GATE_COLS], in_=as_row(a_ln_h_w))
+        nc.gpsimd.dma_start(out=rows[0:1, SHIFT_G : SHIFT_G + GATE_COLS], in_=as_row(a_ln_i_b))
+        nc.gpsimd.dma_start(out=rows[1:2, SHIFT_G : SHIFT_G + GATE_COLS], in_=as_row(a_ln_h_b))
+        nc.gpsimd.dma_start(out=rows[0:1, GAIN_I : GAIN_I + GATE_COLS], in_=as_row(a_ln_i_w))
+        nc.gpsimd.dma_start(out=rows[0:1, GAIN_C : GAIN_C + CELL], in_=as_row(a_ln_c_w))
+        nc.gpsimd.dma_start(out=rows[0:1, SHIFT_C : SHIFT_C + CELL], in_=as_row(a_ln_c_b))
+        ac_sb = keep.tile([P, BATCH_TILES, CELL], BF16)
+        nc.gpsimd.dma_start(out=ac_sb[:], in_=ac.rearrange("(p t) c -> p t c", t=BATCH_TILES))
 
         w_tiles = {}
         first_pass = 0
@@ -237,8 +225,6 @@ def tile_adaptivelstmcell_pa_k_kernel(
             grouped = stage.tile([P, CHUNK_PASSES, P, PACK], BF16, align_bytes=64)
             regroup_chunk(nc, grouped, filled, step * len(filled))
             regrouped = (key, grouped)
-            if step + 1 < PASSES // TILE_PASSES:
-                load_scales(step + 1)
         quantise_chunk(regrouped[0], regrouped[1])
 
         gates = keep.tile([P, BATCH_TILES, GATE_COLS + CELL], F32)
@@ -308,7 +294,7 @@ def tile_adaptivelstmcell_pa_k_kernel(
                     lhsT=ai_codes[key][:, in_chunk].bitcast(FP8X4),
                     lhsT_scale=ai_scales[key][:, in_chunk],
                     rhs=w_tile[:, index, :].bitcast(FP8X4),
-                    rhs_scale=w_planes[g // TILE_PASSES][(g // TILE_PASSES) * PLANE_STEP : P, g % TILE_PASSES, :],
+                    rhs_scale=w_planes[(g % PLANE_PASSES) * PLANE_STEP : P, g // PLANE_PASSES, :],
                     start=(g == 0),
                     stop=(g == PASSES - 1),
                 )

@@ -35,15 +35,17 @@ WORDS_PASS = K_PASS // 2
 
 COPY_ROUND = 4
 
-W_LOADS = (1,) * PASSES
+MIXED_FROM_STEP = 15
+PASSES_A_STEP = 1
+WHOLE_CHUNKS = range(1, 6)
+SMALL_LOADS_A_CHUNK = 5
 
 PLANE_PASSES = 4
 PLANE_STEP = 4
 QUADRANTS = 4
 QUADRANT = P // QUADRANTS
 
-TURN_PASS = 2
-HIDDEN_PASS = 6
+SMALL_WORK_FROM_STEP = 5
 
 GAIN_I = 0
 GAIN_H = GAIN_I + GATE_COLS
@@ -58,7 +60,7 @@ def as_row(vector):
 
 
 def transpose_chunk(nc, banks, ai_tile, ident_words):
-    words = ai_tile[:].bitcast(F32)
+    words = ai_tile.bitcast(F32)
     filled = []
     for half in range(CHUNK_PASSES // BANK_PASSES):
         bank = banks.tile([P, BANK_PASSES, 2, P], F32, tag="bank")
@@ -130,8 +132,8 @@ def tile_adaptivelstmcell_pa_k_kernel(
 ):
     nc = tc.nc
     tiles = range(BATCH_TILES)
-    x_tiles = x.rearrange("(p t) k -> t p k", t=BATCH_TILES)
-    hx_tiles = hx.rearrange("(p t) k -> t p k", t=BATCH_TILES)
+    x_tiles = x.rearrange("(p t) k -> p t k", t=BATCH_TILES)
+    hx_tiles = hx.rearrange("(p t) k -> p t k", t=BATCH_TILES)
     with ExitStack() as ctx:
         ctx.enter_context(tc.manual_schedule())
         keep = ctx.enter_context(tc.tile_pool(name="keep", bufs=1))
@@ -152,56 +154,74 @@ def tile_adaptivelstmcell_pa_k_kernel(
         masks.make_identity(nc, ident_words[:])
         ident_bf16 = keep.tile([P, P], BF16)
         nc.scalar.copy(out=ident_bf16[:], in_=ident_words[:])
-        gate_scale = keep.tile([P, GATE_COLS], F32)
-        nc.vector.memset(gate_scale[:], 0.5)
-        nc.vector.memset(gate_scale[:, 2 * CELL : 3 * CELL], 1.0)
+        halves = keep.tile([P, P], BF16)
+        nc.vector.memset(halves[:], 0.5)
         table_warmer = keep.tile([P, 1], F32)
         nc.scalar.activation(out=table_warmer[:], in_=neg_half[:, 0:1], func=ACT.Tanh)
 
-        def load_scales(quadrant, r):
+        def scale_rows(quadrant, r):
             start = quadrant * QUADRANT + r
-            nc.sync.dma_start(
-                out=w_planes[start : start + PLANE_PASSES * PLANE_STEP : PLANE_STEP, :, :].bitcast(I32),
-                in_=a_w_ih_scales[:, quadrant * PLANE_STEP + r, :]
+            return (
+                w_planes[start : start + PLANE_PASSES * PLANE_STEP : PLANE_STEP, :, :].bitcast(I32),
+                a_w_ih_scales[:, quadrant * PLANE_STEP + r, :]
                 .rearrange("(j i) n -> i j n", i=PLANE_PASSES)
                 .bitcast(I32),
             )
 
-        scale_loads = [(quadrant, r) for quadrant in range(QUADRANTS) for r in range(PLANE_STEP)]
-        ai_tiles = {}
-        for chunk in range(CHUNKS):
-            source = x_tiles if chunk < CHUNKS_IN_X else hx_tiles
-            first = (chunk % CHUNKS_IN_X) * CHUNK_COLS
-            for bt in tiles:
-                ai_tile = keep.tile([P, CHUNK_COLS], BF16, name="ai_%d_%d" % (chunk, bt))
-                nc.sync.dma_start(out=ai_tile[:], in_=source[bt, :, first : first + CHUNK_COLS])
-                ai_tiles[(chunk, bt)] = ai_tile
-                load_scales(*scale_loads[chunk * BATCH_TILES + bt])
+        w_tiles = []
+
+        def load_w():
+            w_tile = keep.tile([P, GATE_COLS], U32, name="w_%d" % len(w_tiles), align_bytes=64)
+            nc.sync.dma_start(
+                out=w_tile[:].bitcast(I32), in_=a_w_ih_words[len(w_tiles)].rearrange("p n t -> p (n t)").bitcast(I32)
+            )
+            w_tiles.append(w_tile)
 
         ah_sb = keep.tile([P, BATCH_TILES, CELL], BF16)
-        nc.gpsimd.dma_start(out=ah_sb[:], in_=ah.rearrange("(p t) k -> p t k", t=BATCH_TILES))
         whh_sb = keep.tile([P, GATE_COLS // P, CELL], BF16)
-        nc.gpsimd.dma_start(out=whh_sb[:], in_=a_w_hh.rearrange("(c p) k -> p c k", p=P))
-        nc.gpsimd.dma_start(out=rows[0:1, GAIN_H : GAIN_H + GATE_COLS], in_=as_row(a_ln_h_w))
-        nc.gpsimd.dma_start(out=rows[0:1, SHIFT_G : SHIFT_G + GATE_COLS], in_=as_row(a_ln_i_b))
-        nc.gpsimd.dma_start(out=rows[1:2, SHIFT_G : SHIFT_G + GATE_COLS], in_=as_row(a_ln_h_b))
-        nc.gpsimd.dma_start(out=rows[0:1, GAIN_I : GAIN_I + GATE_COLS], in_=as_row(a_ln_i_w))
-        nc.gpsimd.dma_start(out=rows[0:1, GAIN_C : GAIN_C + CELL], in_=as_row(a_ln_c_w))
-        nc.gpsimd.dma_start(out=rows[0:1, SHIFT_C : SHIFT_C + CELL], in_=as_row(a_ln_c_b))
         ac_sb = keep.tile([P, BATCH_TILES, CELL], BF16)
-        nc.gpsimd.dma_start(out=ac_sb[:], in_=ac.rearrange("(p t) c -> p t c", t=BATCH_TILES))
+        small_loads = [
+            (ah_sb[:], ah.rearrange("(p t) k -> p t k", t=BATCH_TILES)),
+            (whh_sb[:], a_w_hh.rearrange("(c p) k -> p c k", p=P)),
+            (rows[0:1, GAIN_H : GAIN_H + GATE_COLS], as_row(a_ln_h_w)),
+            (rows[0:1, SHIFT_G : SHIFT_G + GATE_COLS], as_row(a_ln_i_b)),
+            (rows[1:2, SHIFT_G : SHIFT_G + GATE_COLS], as_row(a_ln_h_b)),
+            (rows[0:1, GAIN_I : GAIN_I + GATE_COLS], as_row(a_ln_i_w)),
+            (rows[0:1, GAIN_C : GAIN_C + CELL], as_row(a_ln_c_w)),
+            (rows[0:1, SHIFT_C : SHIFT_C + CELL], as_row(a_ln_c_b)),
+            (ac_sb[:], ac.rearrange("(p t) c -> p t c", t=BATCH_TILES)),
+        ]
+        for quadrant in range(QUADRANTS):
+            for r in range(PLANE_STEP):
+                small_loads.append(scale_rows(quadrant, r))
+        small_loads.reverse()
 
-        w_tiles = {}
-        first_pass = 0
-        for passes in W_LOADS:
-            w_tile = keep.tile([P, passes, GATE_COLS], U32, name="w_%d" % first_pass, align_bytes=64)
-            nc.sync.dma_start(
-                out=w_tile[:].bitcast(I32),
-                in_=a_w_ih_words[first_pass : first_pass + passes].rearrange("g p n t -> p g (n t)").bitcast(I32),
-            )
-            for i in range(passes):
-                w_tiles[first_pass + i] = (w_tile, i)
-            first_pass += passes
+        def some_small_loads(count):
+            for turn in range(min(count, len(small_loads))):
+                out, in_ = small_loads.pop()
+                nc.sync.dma_start(out=out, in_=in_)
+
+        ai_tiles = {}
+        keys = [(chunk, bt) for chunk in range(CHUNKS) for bt in tiles]
+        for chunk in range(CHUNKS):
+            source = x_tiles if chunk < CHUNKS_IN_X else hx_tiles
+            columns = slice((chunk % CHUNKS_IN_X) * CHUNK_COLS, (chunk % CHUNKS_IN_X + 1) * CHUNK_COLS)
+            if chunk in WHOLE_CHUNKS:
+                both = keep.tile([P, BATCH_TILES, CHUNK_COLS], BF16, name="ai_%d" % chunk)
+                nc.sync.dma_start(out=both[:], in_=source[:, :, columns])
+                for bt in tiles:
+                    ai_tiles[(chunk, bt)] = both[:, bt, :]
+                some_small_loads(SMALL_LOADS_A_CHUNK)
+            else:
+                for bt in tiles:
+                    if chunk * BATCH_TILES + bt >= MIXED_FROM_STEP:
+                        for turn in range(PASSES_A_STEP):
+                            load_w()
+                    ai_tile = keep.tile([P, CHUNK_COLS], BF16, name="ai_%d_%d" % (chunk, bt))
+                    nc.sync.dma_start(out=ai_tile[:], in_=source[:, bt, columns])
+                    ai_tiles[(chunk, bt)] = ai_tile[:]
+        while len(w_tiles) < PASSES:
+            load_w()
 
         ai_codes = {}
         ai_scales = {}
@@ -217,17 +237,11 @@ def tile_adaptivelstmcell_pa_k_kernel(
             ai_codes[key] = codes
             ai_scales[key] = scales
 
-        regrouped = None
-        for step, key in enumerate([(chunk, bt) for chunk in range(CHUNKS) for bt in tiles]):
-            filled = transpose_chunk(nc, banks, ai_tiles[key], ident_words)
-            if regrouped is not None:
-                quantise_chunk(regrouped[0], regrouped[1])
-            grouped = stage.tile([P, CHUNK_PASSES, P, PACK], BF16, align_bytes=64)
-            regroup_chunk(nc, grouped, filled, step * len(filled))
-            regrouped = (key, grouped)
-        quantise_chunk(regrouped[0], regrouped[1])
-
         gates = keep.tile([P, BATCH_TILES, GATE_COLS + CELL], F32)
+
+        k_first = keep.tile([P, BATCH_TILES + GATE_COLS // P, P], BF16)
+        spread = keep.tile([P, ROW_COLS], F32)
+        hg = keep.tile([P, BATCH_TILES, GATE_COLS], F32)
 
         def turn_small():
             k_first_ps = banks.tile([P, BATCH_TILES + GATE_COLS // P, P], BF16, tag="bank")
@@ -235,69 +249,94 @@ def tile_adaptivelstmcell_pa_k_kernel(
                 nc.tensor.transpose(out=k_first_ps[:, bt, :], in_=ah_sb[:, bt, :], identity=ident_bf16[:])
             for c in range(GATE_COLS // P):
                 nc.tensor.transpose(out=k_first_ps[:, BATCH_TILES + c, :], in_=whh_sb[:, c, :], identity=ident_bf16[:])
-            k_first = keep.tile([P, BATCH_TILES + GATE_COLS // P, P], BF16)
             nc.scalar.copy(out=k_first[:], in_=k_first_ps[:])
-            nc.scalar.copy(out=gates[:, :, 3 * CELL : 4 * CELL], in_=ac_sb[:])
 
-            spread = keep.tile([P, ROW_COLS], F32)
-            for first in range(0, ROW_COLS, GATE_COLS):
-                width = min(GATE_COLS, ROW_COLS - first)
-                spread_ps = banks.tile([P, GATE_COLS], F32, tag="bank")
+        def spread_rows(first, width):
+            spread_ps = banks.tile([P, GATE_COLS], F32, tag="bank")
+            for part in range(0, width, CELL):
+                halved = first < GAIN_C and part != 2 * CELL
                 nc.tensor.matmul(
-                    out=spread_ps[:, :width], lhsT=ones[:], rhs=rows[:, first : first + width], start=True, stop=True
-                )
-                if first < GAIN_C:
-                    nc.vector.tensor_mul(out=spread[:, first : first + width], in0=spread_ps[:, :width], in1=gate_scale[:])
-                else:
-                    nc.scalar.copy(out=spread[:, first : first + width], in_=spread_ps[:, :width])
-            return k_first, spread
-
-        def hidden_gates():
-            hg_ps = []
-            for bt in tiles:
-                hg = banks.tile([P, GATE_COLS], F32, tag="bank")
-                nc.tensor.matmul(
-                    out=hg[:],
-                    lhsT=k_first[:, bt, :],
-                    rhs=k_first[:, BATCH_TILES:, :].rearrange("p c n -> p (c n)"),
+                    out=spread_ps[:, part : part + CELL],
+                    lhsT=halves[:] if halved else ones[:],
+                    rhs=rows[:, first + part : first + part + CELL],
                     start=True,
                     stop=True,
                 )
-                hg_ps.append(hg[:])
-            mean_var, rstd = moments(nc, small, neg_half, hg_ps, EPS)
-            centred = keep.tile([P, BATCH_TILES, GATE_COLS], F32, tag="centred")
-            hg_shift = keep.tile([P, BATCH_TILES, GATE_COLS], F32)
-            normalise(
-                nc,
-                [hg_shift[:, bt, :] for bt in tiles],
-                centred,
-                hg_ps,
-                mean_var,
-                rstd,
-                spread[:, GAIN_H : GAIN_H + GATE_COLS],
-                [spread[:, SHIFT_G : SHIFT_G + GATE_COLS] for bt in tiles],
+            nc.scalar.copy(out=spread[:, first : first + width], in_=spread_ps[:, :width])
+
+        def hidden_product(bt):
+            hg_ps = banks.tile([P, GATE_COLS], F32, tag="bank")
+            nc.tensor.matmul(
+                out=hg_ps[:],
+                lhsT=k_first[:, bt, :],
+                rhs=k_first[:, BATCH_TILES:, :].rearrange("p c n -> p (c n)"),
+                start=True,
+                stop=True,
             )
-            return hg_shift
+            nc.scalar.copy(out=hg[:, bt, :], in_=hg_ps[:])
+
+        small_work = [
+            turn_small,
+            lambda: spread_rows(GAIN_I, GATE_COLS),
+            lambda: spread_rows(GAIN_H, GATE_COLS),
+            lambda: spread_rows(SHIFT_G, GATE_COLS),
+            lambda: spread_rows(GAIN_C, 2 * CELL),
+            lambda: hidden_product(0),
+            lambda: hidden_product(1),
+            lambda: nc.scalar.copy(out=gates[:, :, 3 * CELL : 4 * CELL], in_=ac_sb[:]),
+        ]
 
         ig_ps = [sums.tile([P, GATE_COLS], F32, name="ig_%d" % bt) for bt in tiles]
-        for g in range(PASSES):
-            if g == TURN_PASS:
-                k_first, spread = turn_small()
-            if g == HIDDEN_PASS:
-                hg_shift = hidden_gates()
-            w_tile, index = w_tiles[g]
+
+        def mx_pass(g, bt):
             in_chunk = slice((g % CHUNK_PASSES) * P, (g % CHUNK_PASSES + 1) * P)
+            key = (g // CHUNK_PASSES, bt)
+            nc.tensor.matmul_mx(
+                out=ig_ps[bt][:],
+                lhsT=ai_codes[key][:, in_chunk].bitcast(FP8X4),
+                lhsT_scale=ai_scales[key][:, in_chunk],
+                rhs=w_tiles[g][:].bitcast(FP8X4),
+                rhs_scale=w_planes[(g % PLANE_PASSES) * PLANE_STEP : P, g // PLANE_PASSES, :],
+                start=(g == 0),
+                stop=(g == PASSES - 1),
+            )
+
+        regrouped = None
+        next_pass = 0
+        for step, key in enumerate(keys):
+            if step >= MIXED_FROM_STEP:
+                for g in range(next_pass, next_pass + PASSES_A_STEP):
+                    for bt in tiles:
+                        mx_pass(g, bt)
+                next_pass += PASSES_A_STEP
+            filled = transpose_chunk(nc, banks, ai_tiles[key], ident_words)
+            if regrouped is not None:
+                quantise_chunk(regrouped[0], regrouped[1])
+            grouped = stage.tile([P, CHUNK_PASSES, P, PACK], BF16, align_bytes=64)
+            regroup_chunk(nc, grouped, filled, step * len(filled))
+            regrouped = (key, grouped)
+            if 0 <= step - SMALL_WORK_FROM_STEP < len(small_work):
+                small_work[step - SMALL_WORK_FROM_STEP]()
+        quantise_chunk(regrouped[0], regrouped[1])
+
+        hgs = [hg[:, bt, :] for bt in tiles]
+        mean_var, rstd = moments(nc, small, neg_half, hgs, EPS)
+        centred = keep.tile([P, BATCH_TILES, GATE_COLS], F32, tag="centred")
+        hg_shift = keep.tile([P, BATCH_TILES, GATE_COLS], F32)
+        normalise(
+            nc,
+            [hg_shift[:, bt, :] for bt in tiles],
+            centred,
+            hgs,
+            mean_var,
+            rstd,
+            spread[:, GAIN_H : GAIN_H + GATE_COLS],
+            [spread[:, SHIFT_G : SHIFT_G + GATE_COLS] for bt in tiles],
+        )
+
+        for g in range(next_pass, PASSES):
             for bt in tiles:
-                key = (g // CHUNK_PASSES, bt)
-                nc.tensor.matmul_mx(
-                    out=ig_ps[bt][:],
-                    lhsT=ai_codes[key][:, in_chunk].bitcast(FP8X4),
-                    lhsT_scale=ai_scales[key][:, in_chunk],
-                    rhs=w_tile[:, index, :].bitcast(FP8X4),
-                    rhs_scale=w_planes[(g % PLANE_PASSES) * PLANE_STEP : P, g // PLANE_PASSES, :],
-                    start=(g == 0),
-                    stop=(g == PASSES - 1),
-                )
+                mx_pass(g, bt)
 
         ig = [ig_ps[bt][:] for bt in tiles]
         mean_var, rstd = moments(nc, small, neg_half, ig, EPS)

@@ -38,7 +38,8 @@ COPY_ROUND = 4
 MIXED_FROM_STEP = 15
 PASSES_A_STEP = 1
 WHOLE_CHUNKS = range(1, 6)
-SMALL_LOADS_A_CHUNK = 5
+SMALL_LOADS_A_CHUNK = 4
+GPSIMD_QUADRANTS = range(2, 4)
 
 PLANE_PASSES = 4
 PLANE_STEP = 4
@@ -193,7 +194,11 @@ def tile_adaptivelstmcell_pa_k_kernel(
         ]
         for quadrant in range(QUADRANTS):
             for r in range(PLANE_STEP):
-                small_loads.append(scale_rows(quadrant, r))
+                out, in_ = scale_rows(quadrant, r)
+                if quadrant in GPSIMD_QUADRANTS:
+                    nc.gpsimd.dma_start(out=out, in_=in_)
+                else:
+                    small_loads.append((out, in_))
         small_loads.reverse()
 
         def some_small_loads(count):

@@ -33,12 +33,10 @@ CHUNKS_IN_X = FEATURES // CHUNK_COLS
 BANK_PASSES = 2
 WORDS_PASS = K_PASS // 2
 
-COPY_ROUND = 4
+VECTOR_COPIES_FROM_STEP = 12
 
-MIXED_FROM_STEP = 15
-PASSES_A_STEP = 1
-WHOLE_CHUNKS = range(1, 6)
-SMALL_LOADS_A_CHUNK = 4
+
+SMALL_LOADS = (0, 0, 2, 2, 2, 2, 1, 1, 1, 1, 1, 1, 1, 1, 1, 0)
 GPSIMD_QUADRANTS = range(2, 4)
 
 PLANE_PASSES = 4
@@ -46,7 +44,7 @@ PLANE_STEP = 4
 QUADRANTS = 4
 QUADRANT = P // QUADRANTS
 
-SMALL_WORK_FROM_STEP = 5
+SMALL_WORK_FROM_STEP = 6
 
 GAIN_I = 0
 GAIN_H = GAIN_I + GATE_COLS
@@ -61,7 +59,7 @@ def as_row(vector):
 
 
 def transpose_chunk(nc, banks, ai_tile, ident_words):
-    words = ai_tile.bitcast(F32)
+    words = ai_tile[:].bitcast(F32)
     filled = []
     for half in range(CHUNK_PASSES // BANK_PASSES):
         bank = banks.tile([P, BANK_PASSES, 2, P], F32, tag="bank")
@@ -77,12 +75,12 @@ def transpose_chunk(nc, banks, ai_tile, ident_words):
     return filled
 
 
-def regroup_chunk(nc, grouped, filled, first_bank):
+def regroup_chunk(nc, grouped, filled, both_engines):
     grouped_words = grouped[:].bitcast(F32)
     for half, bank in enumerate(filled):
         out = grouped_words[:, half * BANK_PASSES : (half + 1) * BANK_PASSES, :, :]
         in_ = bank[:].rearrange("p i u b -> p i b u")
-        if (first_bank + half) % COPY_ROUND == COPY_ROUND - 1:
+        if both_engines and half == 1:
             nc.vector.tensor_copy(out=out, in_=in_)
         else:
             nc.scalar.copy(out=out, in_=in_)
@@ -133,12 +131,12 @@ def tile_adaptivelstmcell_pa_k_kernel(
 ):
     nc = tc.nc
     tiles = range(BATCH_TILES)
-    x_tiles = x.rearrange("(p t) k -> p t k", t=BATCH_TILES)
-    hx_tiles = hx.rearrange("(p t) k -> p t k", t=BATCH_TILES)
+    x_tiles = x.rearrange("(p t) k -> t p k", t=BATCH_TILES)
+    hx_tiles = hx.rearrange("(p t) k -> t p k", t=BATCH_TILES)
     with ExitStack() as ctx:
         ctx.enter_context(tc.manual_schedule())
         keep = ctx.enter_context(tc.tile_pool(name="keep", bufs=1))
-        stage = ctx.enter_context(tc.tile_pool(name="stage", bufs=3))
+        stage = ctx.enter_context(tc.tile_pool(name="stage", bufs=5))
         small = ctx.enter_context(tc.tile_pool(name="small", bufs=4))
         banks = ctx.enter_context(tc.psum_pool(name="banks", bufs=6))
         sums = ctx.enter_context(tc.psum_pool(name="sums", bufs=1))
@@ -171,13 +169,6 @@ def tile_adaptivelstmcell_pa_k_kernel(
 
         w_tiles = []
 
-        def load_w():
-            w_tile = keep.tile([P, GATE_COLS], U32, name="w_%d" % len(w_tiles), align_bytes=64)
-            nc.sync.dma_start(
-                out=w_tile[:].bitcast(I32), in_=a_w_ih_words[len(w_tiles)].rearrange("p n t -> p (n t)").bitcast(I32)
-            )
-            w_tiles.append(w_tile)
-
         ah_sb = keep.tile([P, BATCH_TILES, CELL], BF16)
         whh_sb = keep.tile([P, GATE_COLS // P, CELL], BF16)
         ac_sb = keep.tile([P, BATCH_TILES, CELL], BF16)
@@ -201,32 +192,26 @@ def tile_adaptivelstmcell_pa_k_kernel(
                     small_loads.append((out, in_))
         small_loads.reverse()
 
-        def some_small_loads(count):
-            for turn in range(min(count, len(small_loads))):
-                out, in_ = small_loads.pop()
-                nc.sync.dma_start(out=out, in_=in_)
-
         ai_tiles = {}
         keys = [(chunk, bt) for chunk in range(CHUNKS) for bt in tiles]
-        for chunk in range(CHUNKS):
+        for (chunk, bt), count in zip(keys, SMALL_LOADS):
             source = x_tiles if chunk < CHUNKS_IN_X else hx_tiles
-            columns = slice((chunk % CHUNKS_IN_X) * CHUNK_COLS, (chunk % CHUNKS_IN_X + 1) * CHUNK_COLS)
-            if chunk in WHOLE_CHUNKS:
-                both = keep.tile([P, BATCH_TILES, CHUNK_COLS], BF16, name="ai_%d" % chunk)
-                nc.sync.dma_start(out=both[:], in_=source[:, :, columns])
-                for bt in tiles:
-                    ai_tiles[(chunk, bt)] = both[:, bt, :]
-                some_small_loads(SMALL_LOADS_A_CHUNK)
-            else:
-                for bt in tiles:
-                    if chunk * BATCH_TILES + bt >= MIXED_FROM_STEP:
-                        for turn in range(PASSES_A_STEP):
-                            load_w()
-                    ai_tile = keep.tile([P, CHUNK_COLS], BF16, name="ai_%d_%d" % (chunk, bt))
-                    nc.sync.dma_start(out=ai_tile[:], in_=source[:, bt, columns])
-                    ai_tiles[(chunk, bt)] = ai_tile[:]
-        while len(w_tiles) < PASSES:
-            load_w()
+            first = (chunk % CHUNKS_IN_X) * CHUNK_COLS
+            ai_tile = keep.tile([P, CHUNK_COLS], BF16, name="ai_%d_%d" % (chunk, bt))
+            pieces = 2 if (chunk, bt) == keys[-1] else 1
+            for piece in range(pieces):
+                columns = slice(piece * CHUNK_COLS // pieces, (piece + 1) * CHUNK_COLS // pieces)
+                nc.sync.dma_start(
+                    out=ai_tile[:, columns], in_=source[bt, :, first + columns.start : first + columns.stop]
+                )
+            ai_tiles[(chunk, bt)] = ai_tile
+            for turn in range(count):
+                out, in_ = small_loads.pop()
+                nc.sync.dma_start(out=out, in_=in_)
+        for g in range(PASSES):
+            w_tile = keep.tile([P, GATE_COLS], U32, name="w_%d" % g, align_bytes=64)
+            nc.sync.dma_start(out=w_tile[:].bitcast(I32), in_=a_w_ih_words[g].rearrange("p n t -> p (n t)").bitcast(I32))
+            w_tiles.append(w_tile)
 
         ai_codes = {}
         ai_scales = {}
@@ -306,23 +291,18 @@ def tile_adaptivelstmcell_pa_k_kernel(
                 stop=(g == PASSES - 1),
             )
 
-        regrouped = None
-        next_pass = 0
+        regrouped = []
         for step, key in enumerate(keys):
-            if step >= MIXED_FROM_STEP:
-                for g in range(next_pass, next_pass + PASSES_A_STEP):
-                    for bt in tiles:
-                        mx_pass(g, bt)
-                next_pass += PASSES_A_STEP
             filled = transpose_chunk(nc, banks, ai_tiles[key], ident_words)
-            if regrouped is not None:
-                quantise_chunk(regrouped[0], regrouped[1])
             grouped = stage.tile([P, CHUNK_PASSES, P, PACK], BF16, align_bytes=64)
-            regroup_chunk(nc, grouped, filled, step * len(filled))
-            regrouped = (key, grouped)
+            regroup_chunk(nc, grouped, filled, step >= VECTOR_COPIES_FROM_STEP or step % 2 == 1)
+            if regrouped and step < VECTOR_COPIES_FROM_STEP:
+                quantise_chunk(*regrouped.pop(0))
+            regrouped.append((key, grouped))
             if 0 <= step - SMALL_WORK_FROM_STEP < len(small_work):
                 small_work[step - SMALL_WORK_FROM_STEP]()
-        quantise_chunk(regrouped[0], regrouped[1])
+        for key, grouped in regrouped:
+            quantise_chunk(key, grouped)
 
         hgs = [hg[:, bt, :] for bt in tiles]
         mean_var, rstd = moments(nc, small, neg_half, hgs, EPS)
@@ -339,7 +319,7 @@ def tile_adaptivelstmcell_pa_k_kernel(
             [spread[:, SHIFT_G : SHIFT_G + GATE_COLS] for bt in tiles],
         )
 
-        for g in range(next_pass, PASSES):
+        for g in range(PASSES):
             for bt in tiles:
                 mx_pass(g, bt)
 

@@ -35,9 +35,10 @@ WORDS_PASS = K_PASS // 2
 
 VECTOR_COPIES_FROM_STEP = 12
 
+W_LOADS = (2,) * 10 + (1,) * 12
 
-SMALL_LOADS = (0, 0, 2, 2, 2, 2, 1, 1, 1, 1, 1, 1, 1, 1, 1, 0)
-GPSIMD_QUADRANTS = range(2, 4)
+SMALL_LOADS = (0, 0, 2, 2, 2, 2, 1, 1, 1, 1, 1, 1, 1, 0, 0, 0)
+SYNC_SCALE_LOADS = 6
 
 PLANE_PASSES = 4
 PLANE_STEP = 4
@@ -186,10 +187,10 @@ def tile_adaptivelstmcell_pa_k_kernel(
         for quadrant in range(QUADRANTS):
             for r in range(PLANE_STEP):
                 out, in_ = scale_rows(quadrant, r)
-                if quadrant in GPSIMD_QUADRANTS:
-                    nc.gpsimd.dma_start(out=out, in_=in_)
-                else:
+                if quadrant * PLANE_STEP + r < SYNC_SCALE_LOADS:
                     small_loads.append((out, in_))
+                else:
+                    nc.gpsimd.dma_start(out=out, in_=in_)
         small_loads.reverse()
 
         ai_tiles = {}
@@ -208,10 +209,14 @@ def tile_adaptivelstmcell_pa_k_kernel(
             for turn in range(count):
                 out, in_ = small_loads.pop()
                 nc.sync.dma_start(out=out, in_=in_)
-        for g in range(PASSES):
-            w_tile = keep.tile([P, GATE_COLS], U32, name="w_%d" % g, align_bytes=64)
-            nc.sync.dma_start(out=w_tile[:].bitcast(I32), in_=a_w_ih_words[g].rearrange("p n t -> p (n t)").bitcast(I32))
-            w_tiles.append(w_tile)
+        for passes in W_LOADS:
+            g = len(w_tiles)
+            w_tile = keep.tile([P, passes, GATE_COLS], U32, name="w_%d" % g, align_bytes=64)
+            nc.sync.dma_start(
+                out=w_tile[:].bitcast(I32),
+                in_=a_w_ih_words[g : g + passes].rearrange("g p n t -> p g (n t)").bitcast(I32),
+            )
+            w_tiles.extend([w_tile[:, i, :] for i in range(passes)])
 
         ai_codes = {}
         ai_scales = {}
@@ -285,7 +290,7 @@ def tile_adaptivelstmcell_pa_k_kernel(
                 out=ig_ps[bt][:],
                 lhsT=ai_codes[key][:, in_chunk].bitcast(FP8X4),
                 lhsT_scale=ai_scales[key][:, in_chunk],
-                rhs=w_tiles[g][:].bitcast(FP8X4),
+                rhs=w_tiles[g].bitcast(FP8X4),
                 rhs_scale=w_planes[(g % PLANE_PASSES) * PLANE_STEP : P, g // PLANE_PASSES, :],
                 start=(g == 0),
                 stop=(g == PASSES - 1),

from contextlib import ExitStack

import concourse.masks as masks
import concourse.mybir as mybir

BF16 = mybir.dt.bfloat16
F32 = mybir.dt.float32
I32 = mybir.dt.int32
U32 = mybir.dt.uint32
U8 = mybir.dt.uint8
FP8X4 = mybir.dt.float8_e4m3fn_x4
ALU = mybir.AluOpType
ACT = mybir.ActivationFunctionType

P = 128
BATCH = 256
BATCH_TILES = BATCH // P
FEATURES = 8192
K = 2 * FEATURES
PACK = 4
K_PASS = P * PACK
PASSES = K // K_PASS
GATE_COLS = 512
CELL = 128
EPS = 1e-5

FLOPS = 2 * BATCH * K * GATE_COLS + 2 * BATCH * CELL * GATE_COLS

CHUNK_PASSES = 4
CHUNK_COLS = CHUNK_PASSES * K_PASS
CHUNKS = PASSES // CHUNK_PASSES
CHUNKS_IN_X = FEATURES // CHUNK_COLS
BANK_PASSES = 2
WORDS_PASS = K_PASS // 2

VECTOR_COPIES_FROM_STEP = 12

W_LOADS = (2,) * 10 + (1,) * 12

SMALL_LOADS = (0, 0, 2, 2, 2, 2, 1, 1, 1, 1, 1, 1, 1, 0, 0, 0)
SYNC_SCALE_LOADS = 6

PLANE_PASSES = 4
PLANE_STEP = 4
QUADRANTS = 4
QUADRANT = P // QUADRANTS

SMALL_WORK_FROM_STEP = 6

GAIN_I = 0
GAIN_H = GAIN_I + GATE_COLS
SHIFT_G = GAIN_H + GATE_COLS
GAIN_C = SHIFT_G + GATE_COLS
SHIFT_C = GAIN_C + CELL
ROW_COLS = SHIFT_C + CELL


def as_row(vector):
    return vector.rearrange("(o n) -> o n", o=1)


def transpose_chunk(nc, banks, ai_tile, ident_words):
    words = ai_tile[:].bitcast(F32)
    filled = []
    for half in range(CHUNK_PASSES // BANK_PASSES):
        bank = banks.tile([P, BANK_PASSES, 2, P], F32, tag="bank")
        for i in range(BANK_PASSES):
            first = (half * BANK_PASSES + i) * WORDS_PASS
            for u in range(2):
                nc.tensor.transpose(
                    out=bank[:, i, u, :],
                    in_=words[:, first + u : first + WORDS_PASS : 2],
                    identity=ident_words[:],
                )
        filled.append(bank)
    return filled


def regroup_chunk(nc, grouped, filled, both_engines):
    grouped_words = grouped[:].bitcast(F32)
    for half, bank in enumerate(filled):
        out = grouped_words[:, half * BANK_PASSES : (half + 1) * BANK_PASSES, :, :]
        in_ = bank[:].rearrange("p i u b -> p i b u")
        if both_engines and half == 1:
            nc.vector.tensor_copy(out=out, in_=in_)
        else:
            nc.scalar.copy(out=out, in_=in_)


def moments(nc, small, neg_half, values, eps):
    stats = small.tile([P, BATCH_TILES, 6], F32)
    for bt in range(BATCH_TILES):
        nc.vector.bn_stats(out=stats[:, bt, :], in_=values[bt])
    mean_var = small.tile([P, BATCH_TILES, 2], F32)
    for bt in range(BATCH_TILES):
        nc.vector.bn_aggr(out=mean_var[:, bt, :], in_=stats[:, bt, :])
    var_eps = small.tile([P, BATCH_TILES], F32)
    nc.vector.tensor_scalar_add(out=var_eps[:], in0=mean_var[:, :, 1], scalar1=eps)
    rstd = small.tile([P, BATCH_TILES], F32)
    nc.gpsimd.tensor_tensor(out=rstd[:], in0=var_eps[:], in1=neg_half[:], op=ALU.pow)
    return mean_var, rstd


def normalise(nc, outs, centred, values, mean_var, rstd, gain, shifts):
    for bt in range(BATCH_TILES):
        nc.vector.scalar_tensor_tensor(
            out=centred[:, bt, :], in0=values[bt], scalar=mean_var[:, bt, 0:1], in1=gain, op0=ALU.subtract, op1=ALU.mult
        )
    for bt in range(BATCH_TILES):
        nc.vector.scalar_tensor_tensor(
            out=outs[bt], in0=centred[:, bt, :], scalar=rstd[:, bt : bt + 1], in1=shifts[bt], op0=ALU.mult, op1=ALU.add
        )


def tile_adaptivelstmcell_pa_k_kernel(
    tc,
    x,
    hx,
    ah,
    ac,
    a_w_ih_words,
    a_w_ih_scales,
    a_w_hh,
    a_ln_i_w,
    a_ln_i_b,
    a_ln_h_w,
    a_ln_h_b,
    a_ln_c_w,
    a_ln_c_b,
    out_0,
    out_1,
):
    nc = tc.nc
    tiles = range(BATCH_TILES)
    x_tiles = x.rearrange("(p t) k -> t p k", t=BATCH_TILES)
    hx_tiles = hx.rearrange("(p t) k -> t p k", t=BATCH_TILES)
    with ExitStack() as ctx:
        ctx.enter_context(tc.manual_schedule())
        keep = ctx.enter_context(tc.tile_pool(name="keep", bufs=1))
        stage = ctx.enter_context(tc.tile_pool(name="stage", bufs=5))
        small = ctx.enter_context(tc.tile_pool(name="small", bufs=4))
        banks = ctx.enter_context(tc.psum_pool(name="banks", bufs=6))
        sums = ctx.enter_context(tc.psum_pool(name="sums", bufs=1))

        neg_half = keep.tile([P, BATCH_TILES], F32)
        nc.vector.memset(neg_half[:], -0.5)
        w_planes = keep.tile([P, PASSES // PLANE_PASSES, GATE_COLS], U8, align_bytes=64)
        nc.vector.memset(w_planes[:].bitcast(I32), 0)
        rows = keep.tile([P, ROW_COLS], BF16)
        nc.vector.memset(rows[:], 0.0)
        ones = keep.tile([P, P], BF16)
        nc.vector.memset(ones[:], 1.0)
        ident_words = keep.tile([P, P], F32)
        masks.make_identity(nc, ident_words[:])
        ident_bf16 = keep.tile([P, P], BF16)
        nc.scalar.copy(out=ident_bf16[:], in_=ident_words[:])
        halves = keep.tile([P, P], BF16)
        nc.vector.memset(halves[:], 0.5)
        table_warmer = keep.tile([P, 1], F32)
        nc.scalar.activation(out=table_warmer[:], in_=neg_half[:, 0:1], func=ACT.Tanh)

        def scale_rows(quadrant, r):
            start = quadrant * QUADRANT + r
            return (
                w_planes[start : start + PLANE_PASSES * PLANE_STEP : PLANE_STEP, :, :].bitcast(I32),
                a_w_ih_scales[:, quadrant * PLANE_STEP + r, :]
                .rearrange("(j i) n -> i j n", i=PLANE_PASSES)
                .bitcast(I32),
            )

        w_tiles = []

        ah_sb = keep.tile([P, BATCH_TILES, CELL], BF16)
        whh_sb = keep.tile([P, GATE_COLS // P, CELL], BF16)
        ac_sb = keep.tile([P, BATCH_TILES, CELL], BF16)
        small_loads = [
            (ah_sb[:], ah.rearrange("(p t) k -> p t k", t=BATCH_TILES)),
            (whh_sb[:], a_w_hh.rearrange("(c p) k -> p c k", p=P)),
            (rows[0:1, GAIN_H : GAIN_H + GATE_COLS], as_row(a_ln_h_w)),
            (rows[0:1, SHIFT_G : SHIFT_G + GATE_COLS], as_row(a_ln_i_b)),
            (rows[1:2, SHIFT_G : SHIFT_G + GATE_COLS], as_row(a_ln_h_b)),
            (rows[0:1, GAIN_I : GAIN_I + GATE_COLS], as_row(a_ln_i_w)),
            (rows[0:1, GAIN_C : GAIN_C + CELL], as_row(a_ln_c_w)),
            (rows[0:1, SHIFT_C : SHIFT_C + CELL], as_row(a_ln_c_b)),
            (ac_sb[:], ac.rearrange("(p t) c -> p t c", t=BATCH_TILES)),
        ]
        for quadrant in range(QUADRANTS):
            for r in range(PLANE_STEP):
                out, in_ = scale_rows(quadrant, r)
                if quadrant * PLANE_STEP + r < SYNC_SCALE_LOADS:
                    small_loads.append((out, in_))
                else:
                    nc.gpsimd.dma_start(out=out, in_=in_)
        small_loads.reverse()

        ai_tiles = {}
        keys = [(chunk, bt) for chunk in range(CHUNKS) for bt in tiles]
        for (chunk, bt), count in zip(keys, SMALL_LOADS):
            source = x_tiles if chunk < CHUNKS_IN_X else hx_tiles
            first = (chunk % CHUNKS_IN_X) * CHUNK_COLS
            ai_tile = keep.tile([P, CHUNK_COLS], BF16, name="ai_%d_%d" % (chunk, bt))
            pieces = 2 if (chunk, bt) == keys[-1] else 1
            for piece in range(pieces):
                columns = slice(piece * CHUNK_COLS // pieces, (piece + 1) * CHUNK_COLS // pieces)
                nc.sync.dma_start(
                    out=ai_tile[:, columns], in_=source[bt, :, first + columns.start : first + columns.stop]
                )
            ai_tiles[(chunk, bt)] = ai_tile
            for turn in range(count):
                out, in_ = small_loads.pop()
                nc.sync.dma_start(out=out, in_=in_)
        for passes in W_LOADS:
            g = len(w_tiles)
            w_tile = keep.tile([P, passes, GATE_COLS], U32, name="w_%d" % g, align_bytes=64)
            nc.sync.dma_start(
                out=w_tile[:].bitcast(I32),
                in_=a_w_ih_words[g : g + passes].rearrange("g p n t -> p g (n t)").bitcast(I32),
            )
            w_tiles.extend([w_tile[:, i, :] for i in range(passes)])

        ai_codes = {}
        ai_scales = {}

        def quantise_chunk(key, grouped):
            codes = keep.tile([P, CHUNK_PASSES * P], U32, name="codes_%d_%d" % key, align_bytes=64)
            scales = keep.tile([P, CHUNK_PASSES * P], U8, name="scales_%d_%d" % key, align_bytes=64)
            nc.vector.quantize_mx(
                out=codes[:].bitcast(FP8X4),
                scales=scales[:],
                in_=grouped[:].rearrange("p i b t -> p (i b t)"),
            )
            ai_codes[key] = codes
            ai_scales[key] = scales

        gates = keep.tile([P, BATCH_TILES, GATE_COLS + CELL], F32)

        k_first = keep.tile([P, BATCH_TILES + GATE_COLS // P, P], BF16)
        spread = keep.tile([P, ROW_COLS], F32)
        hg = keep.tile([P, BATCH_TILES, GATE_COLS], F32)

        def turn_small():
            k_first_ps = banks.tile([P, BATCH_TILES + GATE_COLS // P, P], BF16, tag="bank")
            for bt in tiles:
                nc.tensor.transpose(out=k_first_ps[:, bt, :], in_=ah_sb[:, bt, :], identity=ident_bf16[:])
            for c in range(GATE_COLS // P):
                nc.tensor.transpose(out=k_first_ps[:, BATCH_TILES + c, :], in_=whh_sb[:, c, :], identity=ident_bf16[:])
            nc.scalar.copy(out=k_first[:], in_=k_first_ps[:])

        def spread_rows(first, width):
            spread_ps = banks.tile([P, GATE_COLS], F32, tag="bank")
            for part in range(0, width, CELL):
                halved = first < GAIN_C and part != 2 * CELL
                nc.tensor.matmul(
                    out=spread_ps[:, part : part + CELL],
                    lhsT=halves[:] if halved else ones[:],
                    rhs=rows[:, first + part : first + part + CELL],
                    start=True,
                    stop=True,
                )
            nc.scalar.copy(out=spread[:, first : first + width], in_=spread_ps[:, :width])

        def hidden_product(bt):
            hg_ps = banks.tile([P, GATE_COLS], F32, tag="bank")
            nc.tensor.matmul(
                out=hg_ps[:],
                lhsT=k_first[:, bt, :],
                rhs=k_first[:, BATCH_TILES:, :].rearrange("p c n -> p (c n)"),
                start=True,
                stop=True,
            )
            nc.scalar.copy(out=hg[:, bt, :], in_=hg_ps[:])

        small_work = [
            turn_small,
            lambda: spread_rows(GAIN_I, GATE_COLS),
            lambda: spread_rows(GAIN_H, GATE_COLS),
            lambda: spread_rows(SHIFT_G, GATE_COLS),
            lambda: spread_rows(GAIN_C, 2 * CELL),
            lambda: hidden_product(0),
            lambda: hidden_product(1),
            lambda: nc.scalar.copy(out=gates[:, :, 3 * CELL : 4 * CELL], in_=ac_sb[:]),
        ]

        ig_ps = [sums.tile([P, GATE_COLS], F32, name="ig_%d" % bt) for bt in tiles]

        def mx_pass(g, bt):
            in_chunk = slice((g % CHUNK_PASSES) * P, (g % CHUNK_PASSES + 1) * P)
            key = (g // CHUNK_PASSES, bt)
            nc.tensor.matmul_mx(
                out=ig_ps[bt][:],
                lhsT=ai_codes[key][:, in_chunk].bitcast(FP8X4),
                lhsT_scale=ai_scales[key][:, in_chunk],
                rhs=w_tiles[g].bitcast(FP8X4),
                rhs_scale=w_planes[(g % PLANE_PASSES) * PLANE_STEP : P, g // PLANE_PASSES, :],
                start=(g == 0),
                stop=(g == PASSES - 1),
            )

        regrouped = []
        for step, key in enumerate(keys):
            filled = transpose_chunk(nc, banks, ai_tiles[key], ident_words)
            grouped = stage.tile([P, CHUNK_PASSES, P, PACK], BF16, align_bytes=64)
            regroup_chunk(nc, grouped, filled, step >= VECTOR_COPIES_FROM_STEP or step % 2 == 1)
            if regrouped and step < VECTOR_COPIES_FROM_STEP:
                quantise_chunk(*regrouped.pop(0))
            regrouped.append((key, grouped))
            if 0 <= step - SMALL_WORK_FROM_STEP < len(small_work):
                small_work[step - SMALL_WORK_FROM_STEP]()
        for key, grouped in regrouped:
            quantise_chunk(key, grouped)

        hgs = [hg[:, bt, :] for bt in tiles]
        mean_var, rstd = moments(nc, small, neg_half, hgs, EPS)
        centred = keep.tile([P, BATCH_TILES, GATE_COLS], F32, tag="centred")
        hg_shift = keep.tile([P, BATCH_TILES, GATE_COLS], F32)
        normalise(
            nc,
            [hg_shift[:, bt, :] for bt in tiles],
            centred,
            hgs,
            mean_var,
            rstd,
            spread[:, GAIN_H : GAIN_H + GATE_COLS],
            [spread[:, SHIFT_G : SHIFT_G + GATE_COLS] for bt in tiles],
        )

        for g in range(PASSES):
            for bt in tiles:
                mx_pass(g, bt)

        ig = [ig_ps[bt][:] for bt in tiles]
        mean_var, rstd = moments(nc, small, neg_half, ig, EPS)
        centred = keep.tile([P, BATCH_TILES, GATE_COLS], F32, tag="centred")
        for part in (slice(0, 3 * CELL), slice(3 * CELL, GATE_COLS)):
            for bt in tiles:
                nc.vector.scalar_tensor_tensor(
                    out=centred[:, bt, part],
                    in0=ig[bt][:, part],
                    scalar=mean_var[:, bt, 0:1],
                    in1=spread[:, GAIN_I + part.start : GAIN_I + part.stop],
                    op0=ALU.subtract,
                    op1=ALU.mult,
                )
        for part, first in ((slice(0, 3 * CELL), 0), (slice(3 * CELL, GATE_COLS), 4 * CELL)):
            for bt in tiles:
                nc.vector.scalar_tensor_tensor(
                    out=gates[:, bt, first : first + part.stop - part.start],
                    in0=centred[:, bt, part],
                    scalar=rstd[:, bt : bt + 1],
                    in1=hg_shift[:, bt, part],
                    op0=ALU.mult,
                    op1=ALU.add,
                )
        for bt in tiles:
            nc.scalar.activation(out=gates[:, bt, : 3 * CELL], in_=gates[:, bt, : 3 * CELL], func=ACT.Tanh)
        nc.scalar.activation(out=gates[:, :, 4 * CELL :], in_=gates[:, :, 4 * CELL :], func=ACT.Tanh)

        products = keep.tile([P, BATCH_TILES, 2 * CELL], F32)
        twice_cell = keep.tile([P, BATCH_TILES, CELL], F32)
        for bt in tiles:
            nc.vector.scalar_tensor_tensor(
                out=products[:, bt, :],
                in0=gates[:, bt, : 2 * CELL],
                scalar=1.0,
                in1=gates[:, bt, 2 * CELL : 4 * CELL],
                op0=ALU.add,
                op1=ALU.mult,
            )
        for bt in tiles:
            nc.vector.tensor_add(
                out=twice_cell[:, bt, :], in0=products[:, bt, :CELL], in1=products[:, bt, CELL:]
            )
        cells = [twice_cell[:, bt, :] for bt in tiles]
        mean_var, rstd = moments(nc, small, neg_half, cells, 4.0 * EPS)

        sigmoid_o = keep.tile([P, BATCH_TILES, CELL], F32)
        nc.vector.tensor_scalar(
            out=sigmoid_o[:], in0=gates[:, :, 4 * CELL :], scalar1=0.5, scalar2=0.5, op0=ALU.mult, op1=ALU.add
        )

        centred_cell = keep.tile([P, BATCH_TILES, CELL], F32)
        acy = keep.tile([P, BATCH_TILES, CELL], F32)
        normalise(
            nc,
            [acy[:, bt, :] for bt in tiles],
            centred_cell,
            cells,
            mean_var,
            rstd,
            spread[:, GAIN_C : GAIN_C + CELL],
            [spread[:, SHIFT_C : SHIFT_C + CELL] for bt in tiles],
        )
        nc.sync.dma_start(out=out_1.rearrange("(p t) c -> p t c", t=BATCH_TILES), in_=acy[:])
        tanh_acy = keep.tile([P, BATCH_TILES, CELL], F32)
        ada = keep.tile([P, BATCH_TILES, CELL], F32)
        for bt in tiles:
            nc.scalar.activation(out=tanh_acy[:, bt, :], in_=acy[:, bt, :], func=ACT.Tanh)
        for bt in tiles:
            nc.vector.tensor_mul(out=ada[:, bt, :], in0=sigmoid_o[:, bt, :], in1=tanh_acy[:, bt, :])
        nc.sync.dma_start(out=out_0.rearrange("(p t) c -> p t c", t=BATCH_TILES), in_=ada[:])
